import numpy as np
import ml_dtypes


def mxq(x, axis, fmt="e4m3"):
    dtype, down = {"e4m3": (ml_dtypes.float8_e4m3fn, 7), "e5m2": (ml_dtypes.float8_e5m2, 14)}[fmt]
    v = np.moveaxis(np.asarray(x, np.float32).astype(ml_dtypes.bfloat16).astype(np.float64), axis, -1)
    blocks = v.reshape(v.shape[:-1] + (-1, 32))
    amax = np.abs(blocks).max(-1, keepdims=True)
    byte = np.maximum(np.where(amax > 0, np.frexp(amax)[1] - 1 + 127, 0) - down, 1)
    scale = np.exp2(byte - 127.0)
    codes = (blocks / scale).astype(np.float32).astype(dtype).astype(np.float64)
    return np.moveaxis((codes * scale).reshape(v.shape), -1, axis)


WIDE = False


def mx_kscale(k):
    if not WIDE:
        return np.ones(k)
    levels = np.array([10, -10, 5, -5, 0])
    a = np.random.permutation(np.resize(levels, k // 512 * 4)).reshape(k // 512, 4)
    idx = np.arange(k)
    return np.exp2(a[idx // 512, idx % 128 // 32])


BF16 = ml_dtypes.bfloat16


def bf(x):
    return np.asarray(x, np.float32).astype(BF16)


def f64(x):
    return np.asarray(x).astype(np.float64)


B, S, D, E, EV, F, G = 2, 512, 1024, 1024, 1024, 2048, 16
C = D // G
EPS_GN = 1e-5
EPS_L2 = 1e-12


def group_norm(x, gamma, beta):
    xg = x.reshape(B, S, G, C)
    mean = xg.mean(axis=(1, 3), keepdims=True)
    var = np.square(xg - mean).mean(axis=(1, 3), keepdims=True)
    xn = ((xg - mean) / np.sqrt(var + EPS_GN)).reshape(B, S, D)
    return xn * gamma + beta


def l2norm(u):
    n = np.sqrt(np.sum(u * u, axis=-1, keepdims=True))
    return u / np.maximum(n, EPS_L2)


def draw_stream():
    lev = np.repeat(np.random.standard_normal((B, 1, G)) * 0.5, C, axis=2)
    spr = np.repeat(np.random.uniform(0.5, 2.0, (B, 1, G)), C, axis=2)
    return np.random.standard_normal((B, S, D)) * spr + lev


def setup_inputs():
    s = mx_kscale(D)
    w = 1.0 / np.sqrt(D)
    return {"x": bf(draw_stream()),
            "gn1_g": bf((1.0 + 0.1 * np.random.standard_normal(D)) * s),
            "gn1_b": bf(0.3 * np.random.standard_normal(D) * s),
            "wq": bf(np.random.standard_normal((E, D)) * w / s[None, :]),
            "wk": bf(np.random.standard_normal((E, D)) * w / s[None, :]),
            "wv": bf(np.random.standard_normal((EV, D)) * w / s[None, :])}


def reference(x, gn1_g, gn1_b, wq, wk, wv):
    h = group_norm(f64(x), f64(gn1_g), f64(gn1_b))
    hq = mxq(h, 2, "e4m3")
    q = l2norm(hq @ mxq(f64(wq), 1, "e4m3").T)
    k = l2norm(hq @ mxq(f64(wk), 1, "e4m3").T)
    v = hq @ mxq(f64(wv), 1, "e4m3").T
    return q, k, v

@@ -1,0 +1,354 @@
+from contextlib import ExitStack
+
+import concourse.mybir as mybir
+from concourse.masks import make_identity
+
+F32 = mybir.dt.float32
+BF16 = mybir.dt.bfloat16
+U32 = mybir.dt.uint32
+U8 = mybir.dt.uint8
+FP8X4 = mybir.dt.float8_e4m3fn_x4
+ACT = mybir.ActivationFunctionType
+ALU = mybir.AluOpType
+
+P = 128
+BATCH, SEQ, CHAN, OUTS = 2, 512, 1024, 1024
+PACK = 4
+PASSES = CHAN // (P * PACK)
+BLOCKS = CHAN // (2 * P)
+POS_TILES = SEQ // P
+ROW_TILES = OUTS // P
+BANK = 512
+HALVES = OUTS // BANK
+QUAD = 32
+EPS_GN = 1e-5
+EPS_L2 = 1e-12
+
+FLOPS = 2 * BATCH * SEQ * CHAN * 3 * OUTS
+
+
+def tile_retnetblock_pa_kernel(tc, x, gn1_g, gn1_b, wq, wk, wv, out_0, out_1, out_2):
+    nc = tc.nc
+    weights = (wq, wk, wv)
+    outs = (out_0, out_1, out_2)
+
+    with ExitStack() as ctx:
+        const = ctx.enter_context(tc.tile_pool(name="const", bufs=1))
+        keep = ctx.enter_context(tc.tile_pool(name="keep", bufs=1))
+        small = ctx.enter_context(tc.tile_pool(name="small", bufs=6))
+        h_stage = ctx.enter_context(tc.tile_pool(name="h_stage", bufs=2))
+        w_raw = ctx.enter_context(tc.tile_pool(name="w_raw", bufs=2))
+        w_stage = ctx.enter_context(tc.tile_pool(name="w_stage", bufs=8))
+        out_stage = ctx.enter_context(tc.tile_pool(name="out_stage", bufs=6))
+        scrap = ctx.enter_context(tc.tile_pool(name="scrap", bufs=4))
+        sums_low = ctx.enter_context(tc.psum_pool(name="sums_low", bufs=2))
+        ctx.enter_context(tc.manual_schedule())
+
+        x_sb = keep.tile([P, BATCH, POS_TILES, CHAN], BF16)
+        x_words = keep.tile([P, BATCH, BLOCKS, SEQ], F32)
+        h_planes = keep.tile([P, BATCH, PASSES, PACK, SEQ], BF16)
+        h_codes = keep.tile([P, BATCH, PASSES, SEQ], U32, align_bytes=64)
+        h_scales = keep.tile([P, BATCH, PASSES, SEQ], U8, align_bytes=64)
+        w_codes = keep.tile([P, 3, PASSES, OUTS], U32, align_bytes=64)
+        w_scales = keep.tile([P, 3, PASSES, OUTS], U8, align_bytes=64)
+        chunk_stats = keep.tile([P, BATCH, BLOCKS, 2, 6], F32)
+        moments = keep.tile([P, BATCH, BLOCKS, 2], F32)
+        gain = keep.tile([P, BATCH, BLOCKS, 2], F32)
+        shift = keep.tile([P, BATCH, BLOCKS, 2], F32)
+
+        for b in range(BATCH):
+            x_rows = x[b].rearrange("(p j) c -> p j c", j=POS_TILES)
+            for half in range(2):
+                js = slice(2 * half, 2 * half + 2)
+                nc.sync.dma_start(out=x_sb[:, b, js, :], in_=x_rows[:, js, :])
+        affine_rows = const.tile([P, 2 * P], BF16)
+        nc.vector.memset(affine_rows[:], 0.0)
+        nc.sync.dma_start(out=affine_rows[0:BLOCKS, :], in_=gn1_g.rearrange("(a c) -> a c", a=BLOCKS))
+        nc.sync.dma_start(out=affine_rows[BLOCKS : 2 * BLOCKS, :], in_=gn1_b.rearrange("(a c) -> a c", a=BLOCKS))
+        w_sb = []
+
+        def load_w(w):
+            w_sb.append(w_raw.tile([P, ROW_TILES, CHAN], BF16, name="w_sb"))
+            w_rows = weights[w].rearrange("(r p) k -> p r k", p=P)
+            for half in range(HALVES):
+                rs = slice(4 * half, 4 * half + 4)
+                nc.sync.dma_start(out=w_sb[w][:, rs, :], in_=w_rows[:, rs, :])
+
+        load_w(0)
+        load_w(1)
+
+        ident = const.tile([P, P], F32)
+        make_identity(nc, ident[:])
+        group_avg = const.tile([P, P], F32)
+        nc.vector.memset(group_avg[:], 0.0)
+        for q in range(P // QUAD):
+            span = slice(QUAD * q, QUAD * q + QUAD)
+            nc.vector.memset(group_avg[span, span], 1.0 / QUAD)
+        neg_half = const.tile([P, 1], F32)
+        nc.vector.memset(neg_half[:], -0.5)
+        one = const.tile([P, 1], F32)
+        nc.vector.memset(one[:], 1.0)
+        warm = const.tile([P, 1], F32)
+        nc.scalar.activation(out=warm[:], in_=one[:], func=ACT.Sqrt)
+        affine = const.tile([P, 2, BLOCKS, 2], F32)
+
+        def chunk_statistics(b, half):
+            for a in range(BLOCKS):
+                nc.vector.bn_stats(
+                    out=chunk_stats[:, b, a, half, :],
+                    in_=x_words[:, b, a, 256 * half : 256 * half + 256].bitcast(BF16),
+                )
+
+        def partition_moments(b):
+            for a in range(BLOCKS):
+                nc.vector.bn_aggr(
+                    out=moments[:, b, a, :],
+                    in_=chunk_stats[:, b, a, :, :].rearrange("p h s -> p (h s)"),
+                )
+            sq = small.tile([P, BLOCKS], F32, name="sq")
+            nc.vector.tensor_tensor(out=sq[:], in0=moments[:, b, :, 0], in1=moments[:, b, :, 0], op=ALU.mult)
+            nc.vector.tensor_tensor(out=moments[:, b, :, 1], in0=moments[:, b, :, 1], in1=sq[:], op=ALU.add)
+
+        def group_moments(b, bank):
+            nc.tensor.matmul(
+                out=bank, lhsT=group_avg[:], rhs=moments[:, b].rearrange("p a s -> p (a s)"), start=True, stop=True
+            )
+            both = bank.rearrange("p (a s) -> p a s", s=2)
+            mean_sq = small.tile([P, BLOCKS], F32, name="mean_sq")
+            nc.scalar.activation(out=mean_sq[:], in_=both[:, :, 0], func=ACT.Square)
+            return both[:, :, 0], both[:, :, 1], mean_sq
+
+        def group_deviation(square_mean, mean_sq):
+            var = small.tile([P, BLOCKS], F32, name="var")
+            nc.vector.tensor_tensor(out=var[:], in0=square_mean, in1=mean_sq[:], op=ALU.subtract)
+            nc.vector.tensor_scalar(
+                out=var[:], in0=var[:], scalar1=0.0, scalar2=EPS_GN, op0=ALU.max, op1=ALU.add
+            )
+            std = small.tile([P, BLOCKS], F32, name="std")
+            nc.scalar.activation(out=std[:], in_=var[:], func=ACT.Sqrt)
+            return std
+
+        def gain_and_shift(b, mean, std):
+            rstd = small.tile([P, BLOCKS], F32, name="rstd")
+            nc.vector.reciprocal(out=rstd[:], in_=std[:])
+            shape = [P, BLOCKS, 2]
+            nc.vector.tensor_tensor(
+                out=gain[:, b], in0=affine[:, 0], in1=rstd[:].unsqueeze(2).to_broadcast(shape), op=ALU.mult
+            )
+            moved = small.tile(shape, F32, name="moved")
+            nc.vector.tensor_tensor(
+                out=moved[:], in0=gain[:, b], in1=mean.unsqueeze(2).to_broadcast(shape), op=ALU.mult
+            )
+            nc.vector.tensor_tensor(out=shift[:, b], in0=affine[:, 1], in1=moved[:], op=ALU.subtract)
+
+        def normalise(b, a):
+            pairs = x_words[:, b, a, :].bitcast(BF16).rearrange("p (s e) -> p s e", e=2)
+            for e in range(2):
+                nc.vector.tensor_scalar(
+                    out=h_planes[:, b, a // 2, 2 * (a % 2) + e, :],
+                    in0=pairs[:, :, e],
+                    scalar1=gain[:, b, a, e : e + 1],
+                    scalar2=shift[:, b, a, e : e + 1],
+                    op0=ALU.mult,
+                    op1=ALU.add,
+                )
+
+        def regroup_h(b, c):
+            grouped = h_stage.tile([P, SEQ, PACK], BF16, name="h_grouped", align_bytes=64)
+            nc.vector.tensor_copy(
+                out=grouped[:].rearrange("p (n i) t -> p n t i", i=4),
+                in_=h_planes[:, b, c].rearrange("p t (n i) -> p n t i", i=4),
+            )
+            return grouped
+
+        def quantise_h(b, c, grouped):
+            nc.vector.quantize_mx(
+                out=h_codes[:, b, c, :].bitcast(FP8X4),
+                scales=h_scales[:, b, c, :],
+                in_=grouped[:].rearrange("p s t -> p (s t)"),
+            )
+
+        def quantise_w(w, quarter, grouped):
+            half, c = quarter // PASSES, quarter % PASSES
+            cols = slice(BANK * half, BANK * half + BANK)
+            nc.vector.quantize_mx(
+                out=w_codes[:, w, c, cols].bitcast(FP8X4), scales=w_scales[:, w, c, cols], in_=grouped[:]
+            )
+
+        def start_tile(pool, w, b, j):
+            acc = pool.tile([P, HALVES, BANK], F32, name="acc")
+            slots = slice(P * j, P * j + P)
+            for half in range(HALVES):
+                cols = slice(BANK * half, BANK * half + BANK)
+                for c in range(PASSES):
+                    nc.tensor.matmul_mx(
+                        out=acc[:, half, :],
+                        lhsT=h_codes[:, b, c, slots].bitcast(FP8X4),
+                        lhsT_scale=h_scales[:, b, c, slots],
+                        rhs=w_codes[:, w, c, cols].bitcast(FP8X4),
+                        rhs_scale=w_scales[:, w, c, cols],
+                        start=(c == 0),
+                        stop=(c == PASSES - 1),
+                    )
+            if w == 2:
+                return acc, None
+            square_sums = small.tile([P, HALVES], F32, name="square_sums")
+            for half in range(HALVES):
+                squares = scrap.tile([P, BANK], BF16, name="squares")
+                nc.scalar.activation(
+                    out=squares[:],
+                    in_=acc[:, half, :],
+                    func=ACT.Square,
+                    accum_out=square_sums[:, half : half + 1],
+                )
+            total = small.tile([P, 1], F32, name="total")
+            nc.gpsimd.tensor_scalar(
+                out=total[:],
+                in0=square_sums[:, 0:1],
+                scalar1=square_sums[:, 1:2],
+                scalar2=EPS_L2 * EPS_L2,
+                op0=ALU.add,
+                op1=ALU.max,
+            )
+            inverse = small.tile([P, 1], F32, name="inverse")
+            nc.gpsimd.tensor_tensor(out=inverse[:], in0=total[:], in1=neg_half[:], op=ALU.pow)
+            return acc, inverse
+
+        def finish_tile(w, b, j, acc, inverse):
+            result = out_stage.tile([P, HALVES, BANK], F32, name="result")
+            if w == 2:
+                nc.scalar.copy(out=result[:, 0, :], in_=acc[:, 0, :])
+                nc.vector.tensor_copy(out=result[:, 1, :], in_=acc[:, 1, :])
+            elif w == 0 and b == 0:
+                for half in range(HALVES):
+                    nc.scalar.activation(
+                        out=result[:, half, :], in_=acc[:, half, :], func=ACT.Copy, scale=inverse[:, 0:1]
+                    )
+            else:
+                for half in range(HALVES):
+                    nc.vector.tensor_scalar(
+                        out=result[:, half, :],
+                        in0=acc[:, half, :],
+                        scalar1=inverse[:, 0:1],
+                        scalar2=None,
+                        op0=ALU.mult,
+                    )
+            out_rows = outs[w][b].rearrange("(p j) o -> j p o", j=POS_TILES)
+            nc.sync.dma_start(out=out_rows[j], in_=result[:].rearrange("p h o -> p (h o)"))
+
+        staged = {}
+        with tc.psum_pool(name="flip", bufs=4) as flip:
+
+            def x_to_words(b, j):
+                x_t = flip.tile([P, BANK], F32, name="x_t", tag="flip")
+                words = x_sb[:, b, j, :].bitcast(F32)
+                for a in range(BLOCKS):
+                    cols = slice(P * a, P * a + P)
+                    nc.tensor.transpose(x_t[:, cols], words[:, cols], ident[:])
+                nc.scalar.copy(
+                    out=x_words[:, b, :, P * j : P * j + P],
+                    in_=x_t[:].rearrange("p (a s) -> p a s", a=BLOCKS),
+                )
+
+            def flip_w(w, quarter):
+                half, c = quarter // PASSES, quarter % PASSES
+                grouped = w_stage.tile([P, BANK * PACK], BF16, name="w_grouped", align_bytes=64)
+                grouped_words = grouped[:].bitcast(F32).rearrange("p (o u) -> p o u", u=2)
+                for pair in range(2):
+                    w_t = flip.tile([P, BANK], F32, name="w_t", tag="flip")
+                    for u in range(2):
+                        for i in range(2):
+                            words = w_sb[w][:, 4 * half + 2 * pair + i, :].bitcast(F32)
+                            a = 2 * c + u
+                            nc.tensor.transpose(
+                                w_t[:, 256 * u + P * i : 256 * u + P * i + P],
+                                words[:, P * a : P * a + P],
+                                ident[:],
+                            )
+                    nc.scalar.copy(
+                        out=grouped_words[:, 256 * pair : 256 * pair + 256, :],
+                        in_=w_t[:].rearrange("p (u o) -> p o u", u=2),
+                    )
+                staged[w, quarter] = grouped
+
+            for j in range(POS_TILES):
+                x_to_words(0, j)
+                if j % 2 == 1:
+                    chunk_statistics(0, j // 2)
+            for j in range(POS_TILES):
+                x_to_words(1, j)
+            affine_t = flip.tile([P, BANK], F32, name="affine_t", tag="flip")
+            nc.tensor.transpose(affine_t[:, 0:P], affine_rows[:].bitcast(F32), ident[:])
+            nc.vector.tensor_copy(
+                out=affine[:].rearrange("p s a e -> p (s a e)"),
+                in_=affine_t[:, 0 : 2 * BLOCKS].bitcast(BF16),
+            )
+            partition_moments(0)
+            flip_w(0, 0)
+            flip_w(0, 1)
+            group_t = flip.tile([P, BANK], F32, name="group_t", tag="flip")
+            mean, square_mean, mean_sq = group_moments(0, group_t[:, 0 : 2 * BLOCKS])
+            flip_w(0, 2)
+            chunk_statistics(1, 0)
+            std = group_deviation(square_mean, mean_sq)
+            flip_w(0, 3)
+            load_w(2)
+            quantise_w(0, 0, staged[0, 0])
+            quantise_w(0, 1, staged[0, 1])
+            gain_and_shift(0, mean, std)
+            for quarter in range(4):
+                flip_w(1, quarter)
+            normalise(0, 0)
+            normalise(0, 1)
+            grouped_0 = regroup_h(0, 0)
+            normalise(0, 2)
+            normalise(0, 3)
+            quantise_h(0, 0, grouped_0)
+            grouped_1 = regroup_h(0, 1)
+            quantise_w(0, 2, staged[0, 2])
+            quantise_h(0, 1, grouped_1)
+            quantise_w(0, 3, staged[0, 3])
+            for quarter in range(4):
+                flip_w(2, quarter)
+        sums_high = ctx.enter_context(tc.psum_pool(name="sums_high", bufs=2, reuse_waits="tile"))
+
+        tiles = [(0, 0, j) for j in range(POS_TILES)]
+        tiles.extend([(w, 0, j) for j in range(POS_TILES) for w in (1, 2)])
+        tiles.extend([(w, 1, j) for j in range(POS_TILES) for w in (0, 1, 2)])
+        started = []
+
+        def advance(n):
+            pool = (sums_low, sums_high)[n % 2]
+            started.append(start_tile(pool, *tiles[n]))
+            if n > 0:
+                finish_tile(*tiles[n - 1], *started[n - 1])
+
+        chunk_statistics(1, 1)
+        partition_moments(1)
+        for quarter in range(4):
+            quantise_w(1, quarter, staged[1, quarter])
+        advance(0)
+        advance(1)
+        group_t = sums_low.tile([P, HALVES, BANK], F32, name="acc")
+        mean, square_mean, mean_sq = group_moments(1, group_t[:, 0, 0 : 2 * BLOCKS])
+        quantise_w(2, 0, staged[2, 0])
+        quantise_w(2, 1, staged[2, 1])
+        std = group_deviation(square_mean, mean_sq)
+        quantise_w(2, 2, staged[2, 2])
+        quantise_w(2, 3, staged[2, 3])
+        gain_and_shift(1, mean, std)
+        advance(2)
+        advance(3)
+        normalise(1, 0)
+        normalise(1, 1)
+        grouped_0 = regroup_h(1, 0)
+        normalise(1, 2)
+        normalise(1, 3)
+        quantise_h(1, 0, grouped_0)
+        grouped_1 = regroup_h(1, 1)
+        advance(4)
+        quantise_h(1, 1, grouped_1)
+
+        for n in range(5, len(tiles)):
+            advance(n)
+        finish_tile(*tiles[-1], *started[-1])

@@ -84,12 +84,10 @@ def tile_retnetblock_pa_kernel(tc, x, gn1_g, gn1_b, wq, wk, wv, out_0, out_1, ou
         for q in range(P // QUAD):
             span = slice(QUAD * q, QUAD * q + QUAD)
             nc.vector.memset(group_avg[span, span], 1.0 / QUAD)
-        neg_half = const.tile([P, 1], F32)
-        nc.vector.memset(neg_half[:], -0.5)
-        one = const.tile([P, 1], F32)
-        nc.vector.memset(one[:], 1.0)
+        eps_gn = const.tile([P, 1], F32)
+        nc.vector.memset(eps_gn[:], EPS_GN)
         warm = const.tile([P, 1], F32)
-        nc.scalar.activation(out=warm[:], in_=one[:], func=ACT.Sqrt)
+        nc.scalar.activation(out=warm[:], in_=eps_gn[:], func=ACT.Abs_reciprocal_sqrt)
         affine = const.tile([P, 2, BLOCKS, 2], F32)
 
         def chunk_statistics(b, half):
@@ -118,19 +116,14 @@ def tile_retnetblock_pa_kernel(tc, x, gn1_g, gn1_b, wq, wk, wv, out_0, out_1, ou
             nc.scalar.activation(out=mean_sq[:], in_=both[:, :, 0], func=ACT.Square)
             return both[:, :, 0], both[:, :, 1], mean_sq
 
-        def group_deviation(square_mean, mean_sq):
+        def group_rstd(square_mean, mean_sq):
             var = small.tile([P, BLOCKS], F32, name="var")
             nc.vector.tensor_tensor(out=var[:], in0=square_mean, in1=mean_sq[:], op=ALU.subtract)
-            nc.vector.tensor_scalar(
-                out=var[:], in0=var[:], scalar1=0.0, scalar2=EPS_GN, op0=ALU.max, op1=ALU.add
-            )
-            std = small.tile([P, BLOCKS], F32, name="std")
-            nc.scalar.activation(out=std[:], in_=var[:], func=ACT.Sqrt)
-            return std
-
-        def gain_and_shift(b, mean, std):
             rstd = small.tile([P, BLOCKS], F32, name="rstd")
-            nc.vector.reciprocal(out=rstd[:], in_=std[:])
+            nc.scalar.activation(out=rstd[:], in_=var[:], func=ACT.Abs_reciprocal_sqrt, bias=eps_gn[:, 0:1])
+            return rstd
+
+        def gain_and_shift(b, mean, rstd):
             shape = [P, BLOCKS, 2]
             nc.vector.tensor_tensor(
                 out=gain[:, b], in0=affine[:, 0], in1=rstd[:].unsqueeze(2).to_broadcast(shape), op=ALU.mult
@@ -175,8 +168,15 @@ def tile_retnetblock_pa_kernel(tc, x, gn1_g, gn1_b, wq, wk, wv, out_0, out_1, ou
                 out=w_codes[:, w, c, cols].bitcast(FP8X4), scales=w_scales[:, w, c, cols], in_=grouped[:]
             )
 
-        def start_tile(pool, w, b, j):
+        tiles = [(0, 0, j) for j in range(POS_TILES)]
+        tiles.extend([(w, 0, j) for j in range(POS_TILES) for w in (1, 2)])
+        tiles.extend([(w, 1, j) for j in range(POS_TILES) for w in (0, 1, 2)])
+        accs, square_sums, inverses, results = [], [], [], []
+
+        def start_tile(n, pool):
+            w, b, j = tiles[n]
             acc = pool.tile([P, HALVES, BANK], F32, name="acc")
+            accs.append(acc)
             slots = slice(P * j, P * j + P)
             for half in range(HALVES):
                 cols = slice(BANK * half, BANK * half + BANK)
@@ -190,51 +190,50 @@ def tile_retnetblock_pa_kernel(tc, x, gn1_g, gn1_b, wq, wk, wv, out_0, out_1, ou
                         start=(c == 0),
                         stop=(c == PASSES - 1),
                     )
-            if w == 2:
-                return acc, None
-            square_sums = small.tile([P, HALVES], F32, name="square_sums")
-            for half in range(HALVES):
-                squares = scrap.tile([P, BANK], BF16, name="squares")
-                nc.scalar.activation(
-                    out=squares[:],
-                    in_=acc[:, half, :],
-                    func=ACT.Square,
-                    accum_out=square_sums[:, half : half + 1],
-                )
-            total = small.tile([P, 1], F32, name="total")
-            nc.gpsimd.tensor_scalar(
-                out=total[:],
-                in0=square_sums[:, 0:1],
-                scalar1=square_sums[:, 1:2],
-                scalar2=EPS_L2 * EPS_L2,
-                op0=ALU.add,
-                op1=ALU.max,
-            )
-            inverse = small.tile([P, 1], F32, name="inverse")
-            nc.gpsimd.tensor_tensor(out=inverse[:], in0=total[:], in1=neg_half[:], op=ALU.pow)
-            return acc, inverse
-
-        def finish_tile(w, b, j, acc, inverse):
-            result = out_stage.tile([P, HALVES, BANK], F32, name="result")
-            if w == 2:
-                nc.scalar.copy(out=result[:, 0, :], in_=acc[:, 0, :])
-                nc.vector.tensor_copy(out=result[:, 1, :], in_=acc[:, 1, :])
-            elif w == 0 and b == 0:
+            square_sums.append(small.tile([P, HALVES], F32, name="square_sums") if w < 2 else None)
+            if w < 2:
                 for half in range(HALVES):
+                    squares = scrap.tile([P, BANK], BF16, name="squares")
                     nc.scalar.activation(
-                        out=result[:, half, :], in_=acc[:, half, :], func=ACT.Copy, scale=inverse[:, 0:1]
+                        out=squares[:],
+                        in_=acc[:, half, :],
+                        func=ACT.Square,
+                        accum_out=square_sums[n][:, half : half + 1],
                     )
+
+        def inverse_norm(n):
+            inverses.append(small.tile([P, 1], F32, name="inverse") if tiles[n][0] < 2 else None)
+            if tiles[n][0] < 2:
+                raw = small.tile([P, 1], F32, name="raw")
+                nc.scalar.activation(
+                    out=raw[:],
+                    in_=square_sums[n][:, 0:1],
+                    func=ACT.Abs_reciprocal_sqrt,
+                    bias=square_sums[n][:, 1:2],
+                )
+                nc.vector.tensor_scalar_min(out=inverses[n][:], in0=raw[:], scalar1=1.0 / EPS_L2)
+
+        def leave_psum(n, half):
+            w, b, j = tiles[n]
+            if half == 0:
+                results.append(out_stage.tile([P, HALVES, BANK], F32, name="result"))
+            if w < 2:
+                nc.vector.tensor_scalar(
+                    out=results[n][:, half, :],
+                    in0=accs[n][:, half, :],
+                    scalar1=inverses[n][:, 0:1],
+                    scalar2=None,
+                    op0=ALU.mult,
+                )
+            elif half == 0 or b == 0:
+                nc.scalar.copy(out=results[n][:, half, :], in_=accs[n][:, half, :])
             else:
-                for half in range(HALVES):
-                    nc.vector.tensor_scalar(
-                        out=result[:, half, :],
-                        in0=acc[:, half, :],
-                        scalar1=inverse[:, 0:1],
-                        scalar2=None,
-                        op0=ALU.mult,
-                    )
+                nc.vector.tensor_copy(out=results[n][:, half, :], in_=accs[n][:, half, :])
+
+        def store(n):
+            w, b, j = tiles[n]
             out_rows = outs[w][b].rearrange("(p j) o -> j p o", j=POS_TILES)
-            nc.sync.dma_start(out=out_rows[j], in_=result[:].rearrange("p h o -> p (h o)"))
+            nc.sync.dma_start(out=out_rows[j], in_=results[n][:].rearrange("p h o -> p (h o)"))
 
         staged = {}
         with tc.psum_pool(name="flip", bufs=4) as flip:
@@ -290,12 +289,12 @@ def tile_retnetblock_pa_kernel(tc, x, gn1_g, gn1_b, wq, wk, wv, out_0, out_1, ou
             mean, square_mean, mean_sq = group_moments(0, group_t[:, 0 : 2 * BLOCKS])
             flip_w(0, 2)
             chunk_statistics(1, 0)
-            std = group_deviation(square_mean, mean_sq)
+            rstd = group_rstd(square_mean, mean_sq)
             flip_w(0, 3)
             load_w(2)
             quantise_w(0, 0, staged[0, 0])
             quantise_w(0, 1, staged[0, 1])
-            gain_and_shift(0, mean, std)
+            gain_and_shift(0, mean, rstd)
             for quarter in range(4):
                 flip_w(1, quarter)
             normalise(0, 0)
@@ -310,45 +309,38 @@ def tile_retnetblock_pa_kernel(tc, x, gn1_g, gn1_b, wq, wk, wv, out_0, out_1, ou
             quantise_w(0, 3, staged[0, 3])
             for quarter in range(4):
                 flip_w(2, quarter)
+            chunk_statistics(1, 1)
+            partition_moments(1)
+            group_t = flip.tile([P, BANK], F32, name="group_t", tag="flip")
+            mean, square_mean, mean_sq = group_moments(1, group_t[:, 0 : 2 * BLOCKS])
+            quantise_w(1, 0, staged[1, 0])
+            quantise_w(1, 1, staged[1, 1])
+            rstd = group_rstd(square_mean, mean_sq)
+            quantise_w(1, 2, staged[1, 2])
+            quantise_w(1, 3, staged[1, 3])
+            gain_and_shift(1, mean, rstd)
         sums_high = ctx.enter_context(tc.psum_pool(name="sums_high", bufs=2, reuse_waits="tile"))
-
-        tiles = [(0, 0, j) for j in range(POS_TILES)]
-        tiles.extend([(w, 0, j) for j in range(POS_TILES) for w in (1, 2)])
-        tiles.extend([(w, 1, j) for j in range(POS_TILES) for w in (0, 1, 2)])
-        started = []
+        for quarter in range(4):
+            quantise_w(2, quarter, staged[2, quarter])
 
         def advance(n):
-            pool = (sums_low, sums_high)[n % 2]
-            started.append(start_tile(pool, *tiles[n]))
+            if n < len(tiles):
+                start_tile(n, (sums_low, sums_high)[n % 2])
             if n > 0:
-                finish_tile(*tiles[n - 1], *started[n - 1])
+                leave_psum(n - 1, 0)
+            if n < len(tiles):
+                inverse_norm(n)
+            if n > 0:
+                leave_psum(n - 1, 1)
+                store(n - 1)
 
-        chunk_statistics(1, 1)
-        partition_moments(1)
-        for quarter in range(4):
-            quantise_w(1, quarter, staged[1, quarter])
-        advance(0)
-        advance(1)
-        group_t = sums_low.tile([P, HALVES, BANK], F32, name="acc")
-        mean, square_mean, mean_sq = group_moments(1, group_t[:, 0, 0 : 2 * BLOCKS])
-        quantise_w(2, 0, staged[2, 0])
-        quantise_w(2, 1, staged[2, 1])
-        std = group_deviation(square_mean, mean_sq)
-        quantise_w(2, 2, staged[2, 2])
-        quantise_w(2, 3, staged[2, 3])
-        gain_and_shift(1, mean, std)
-        advance(2)
-        advance(3)
-        normalise(1, 0)
-        normalise(1, 1)
+        for n in range(POS_TILES):
+            advance(n)
+            normalise(1, n)
         grouped_0 = regroup_h(1, 0)
-        normalise(1, 2)
-        normalise(1, 3)
-        quantise_h(1, 0, grouped_0)
         grouped_1 = regroup_h(1, 1)
-        advance(4)
+        quantise_h(1, 0, grouped_0)
         quantise_h(1, 1, grouped_1)
 
-        for n in range(5, len(tiles)):
+        for n in range(POS_TILES, len(tiles) + 1):
             advance(n)
-        finish_tile(*tiles[-1], *started[-1])

@@ -134,10 +134,10 @@ def tile_retnetblock_pa_kernel(tc, x, gn1_g, gn1_b, wq, wk, wv, out_0, out_1, ou
             )
             nc.vector.tensor_tensor(out=shift[:, b], in0=affine[:, 1], in1=moved[:], op=ALU.subtract)
 
-        def normalise(b, a):
+        def normalise(engine, b, a):
             pairs = x_words[:, b, a, :].bitcast(BF16).rearrange("p (s e) -> p s e", e=2)
             for e in range(2):
-                nc.vector.tensor_scalar(
+                engine.tensor_scalar(
                     out=h_planes[:, b, a // 2, 2 * (a % 2) + e, :],
                     in0=pairs[:, :, e],
                     scalar1=gain[:, b, a, e : e + 1],
@@ -168,8 +168,7 @@ def tile_retnetblock_pa_kernel(tc, x, gn1_g, gn1_b, wq, wk, wv, out_0, out_1, ou
                 out=w_codes[:, w, c, cols].bitcast(FP8X4), scales=w_scales[:, w, c, cols], in_=grouped[:]
             )
 
-        tiles = [(0, 0, j) for j in range(POS_TILES)]
-        tiles.extend([(w, 0, j) for j in range(POS_TILES) for w in (1, 2)])
+        tiles = [(w, 0, j) for w in (0, 2, 1) for j in range(POS_TILES)]
         tiles.extend([(w, 1, j) for j in range(POS_TILES) for w in (0, 1, 2)])
         accs, square_sums, inverses, results = [], [], [], []
 
@@ -297,11 +296,11 @@ def tile_retnetblock_pa_kernel(tc, x, gn1_g, gn1_b, wq, wk, wv, out_0, out_1, ou
             gain_and_shift(0, mean, rstd)
             for quarter in range(4):
                 flip_w(1, quarter)
-            normalise(0, 0)
-            normalise(0, 1)
+            normalise(nc.vector, 0, 0)
+            normalise(nc.vector, 0, 1)
             grouped_0 = regroup_h(0, 0)
-            normalise(0, 2)
-            normalise(0, 3)
+            normalise(nc.vector, 0, 2)
+            normalise(nc.vector, 0, 3)
             quantise_h(0, 0, grouped_0)
             grouped_1 = regroup_h(0, 1)
             quantise_w(0, 2, staged[0, 2])
@@ -311,36 +310,36 @@ def tile_retnetblock_pa_kernel(tc, x, gn1_g, gn1_b, wq, wk, wv, out_0, out_1, ou
                 flip_w(2, quarter)
             chunk_statistics(1, 1)
             partition_moments(1)
+            start_tile(0, sums_low)
             group_t = flip.tile([P, BANK], F32, name="group_t", tag="flip")
             mean, square_mean, mean_sq = group_moments(1, group_t[:, 0 : 2 * BLOCKS])
-            quantise_w(1, 0, staged[1, 0])
-            quantise_w(1, 1, staged[1, 1])
+            quantise_w(2, 0, staged[2, 0])
+            quantise_w(2, 1, staged[2, 1])
             rstd = group_rstd(square_mean, mean_sq)
-            quantise_w(1, 2, staged[1, 2])
-            quantise_w(1, 3, staged[1, 3])
+            quantise_w(2, 2, staged[2, 2])
+            quantise_w(2, 3, staged[2, 3])
             gain_and_shift(1, mean, rstd)
         sums_high = ctx.enter_context(tc.psum_pool(name="sums_high", bufs=2, reuse_waits="tile"))
-        for quarter in range(4):
-            quantise_w(2, quarter, staged[2, quarter])
 
         def advance(n):
             if n < len(tiles):
                 start_tile(n, (sums_low, sums_high)[n % 2])
-            if n > 0:
-                leave_psum(n - 1, 0)
+            leave_psum(n - 1, 0)
             if n < len(tiles):
                 inverse_norm(n)
-            if n > 0:
-                leave_psum(n - 1, 1)
-                store(n - 1)
+            leave_psum(n - 1, 1)
+            store(n - 1)
 
-        for n in range(POS_TILES):
-            advance(n)
-            normalise(1, n)
+        inverse_norm(0)
+        for a in range(BLOCKS):
+            advance(1 + a)
+            normalise(nc.gpsimd, 1, a)
+        for quarter in range(4):
+            quantise_w(1, quarter, staged[1, quarter])
         grouped_0 = regroup_h(1, 0)
         grouped_1 = regroup_h(1, 1)
         quantise_h(1, 0, grouped_0)
         quantise_h(1, 1, grouped_1)
 
-        for n in range(POS_TILES, len(tiles) + 1):
+        for n in range(1 + BLOCKS, len(tiles) + 1):
             advance(n)

@@ -41,26 +41,33 @@ def tile_retnetblock_pa_kernel(tc, x, gn1_g, gn1_b, wq, wk, wv, out_0, out_1, ou
         w_stage = ctx.enter_context(tc.tile_pool(name="w_stage", bufs=8))
         out_stage = ctx.enter_context(tc.tile_pool(name="out_stage", bufs=6))
         scrap = ctx.enter_context(tc.tile_pool(name="scrap", bufs=4))
-        sums_low = ctx.enter_context(tc.psum_pool(name="sums_low", bufs=2))
+        sums_low = ctx.enter_context(tc.psum_pool(name="sums_low", bufs=4))
         ctx.enter_context(tc.manual_schedule())
 
-        x_sb = keep.tile([P, BATCH, POS_TILES, CHAN], BF16)
-        x_words = keep.tile([P, BATCH, BLOCKS, SEQ], F32)
-        h_planes = keep.tile([P, BATCH, PASSES, PACK, SEQ], BF16)
-        h_codes = keep.tile([P, BATCH, PASSES, SEQ], U32, align_bytes=64)
-        h_scales = keep.tile([P, BATCH, PASSES, SEQ], U8, align_bytes=64)
-        w_codes = keep.tile([P, 3, PASSES, OUTS], U32, align_bytes=64)
-        w_scales = keep.tile([P, 3, PASSES, OUTS], U8, align_bytes=64)
-        chunk_stats = keep.tile([P, BATCH, BLOCKS, 2, 6], F32)
-        moments = keep.tile([P, BATCH, BLOCKS, 2], F32)
-        gain = keep.tile([P, BATCH, BLOCKS, 2], F32)
-        shift = keep.tile([P, BATCH, BLOCKS, 2], F32)
+        batches = range(BATCH)
+        x_sb = [keep.tile([P, POS_TILES, CHAN], BF16, name="x_sb%d" % b) for b in batches]
+        x_words = [keep.tile([P, POS_TILES, BLOCKS, P], F32, name="x_words%d" % b) for b in batches]
+        chunk_stats = [keep.tile([P, BLOCKS, 2, 6], F32, name="chunk_stats%d" % b) for b in batches]
+        moments = [keep.tile([P, BLOCKS, 2], F32, name="moments%d" % b) for b in batches]
+        gain = [keep.tile([P, BLOCKS, 2], F32, name="gain%d" % b) for b in batches]
+        shift = [keep.tile([P, BLOCKS, 2], F32, name="shift%d" % b) for b in batches]
+        h_planes, h_codes, h_scales = {}, {}, {}
+        for b in batches:
+            for c in range(PASSES):
+                h_planes[b, c] = keep.tile([P, PACK, SEQ], BF16, name="h_planes%d%d" % (b, c))
+                h_codes[b, c] = keep.tile([P, SEQ], U32, name="h_codes%d%d" % (b, c), align_bytes=64)
+                h_scales[b, c] = keep.tile([P, SEQ], U8, name="h_scales%d%d" % (b, c), align_bytes=64)
+        w_codes, w_scales = {}, {}
+        for w in range(3):
+            for quarter in range(4):
+                w_codes[w, quarter] = keep.tile([P, BANK], U32, name="w_codes%d%d" % (w, quarter), align_bytes=64)
+                w_scales[w, quarter] = keep.tile([P, BANK], U8, name="w_scales%d%d" % (w, quarter), align_bytes=64)
 
         for b in range(BATCH):
             x_rows = x[b].rearrange("(p j) c -> p j c", j=POS_TILES)
             for half in range(2):
                 js = slice(2 * half, 2 * half + 2)
-                nc.sync.dma_start(out=x_sb[:, b, js, :], in_=x_rows[:, js, :])
+                nc.sync.dma_start(out=x_sb[b][:, js, :], in_=x_rows[:, js, :])
         affine_rows = const.tile([P, 2 * P], BF16)
         nc.vector.memset(affine_rows[:], 0.0)
         nc.sync.dma_start(out=affine_rows[0:BLOCKS, :], in_=gn1_g.rearrange("(a c) -> a c", a=BLOCKS))
@@ -93,23 +100,23 @@ def tile_retnetblock_pa_kernel(tc, x, gn1_g, gn1_b, wq, wk, wv, out_0, out_1, ou
         def chunk_statistics(b, half):
             for a in range(BLOCKS):
                 nc.vector.bn_stats(
-                    out=chunk_stats[:, b, a, half, :],
-                    in_=x_words[:, b, a, 256 * half : 256 * half + 256].bitcast(BF16),
+                    out=chunk_stats[b][:, a, half, :],
+                    in_=x_words[b][:, 2 * half : 2 * half + 2, a, :].bitcast(BF16),
                 )
 
         def partition_moments(b):
             for a in range(BLOCKS):
                 nc.vector.bn_aggr(
-                    out=moments[:, b, a, :],
-                    in_=chunk_stats[:, b, a, :, :].rearrange("p h s -> p (h s)"),
+                    out=moments[b][:, a, :],
+                    in_=chunk_stats[b][:, a, :, :].rearrange("p h s -> p (h s)"),
                 )
             sq = small.tile([P, BLOCKS], F32, name="sq")
-            nc.vector.tensor_tensor(out=sq[:], in0=moments[:, b, :, 0], in1=moments[:, b, :, 0], op=ALU.mult)
-            nc.vector.tensor_tensor(out=moments[:, b, :, 1], in0=moments[:, b, :, 1], in1=sq[:], op=ALU.add)
+            nc.vector.tensor_tensor(out=sq[:], in0=moments[b][:, :, 0], in1=moments[b][:, :, 0], op=ALU.mult)
+            nc.vector.tensor_tensor(out=moments[b][:, :, 1], in0=moments[b][:, :, 1], in1=sq[:], op=ALU.add)
 
         def group_moments(b, bank):
             nc.tensor.matmul(
-                out=bank, lhsT=group_avg[:], rhs=moments[:, b].rearrange("p a s -> p (a s)"), start=True, stop=True
+                out=bank, lhsT=group_avg[:], rhs=moments[b][:].rearrange("p a s -> p (a s)"), start=True, stop=True
             )
             both = bank.rearrange("p (a s) -> p a s", s=2)
             mean_sq = small.tile([P, BLOCKS], F32, name="mean_sq")
@@ -126,22 +133,22 @@ def tile_retnetblock_pa_kernel(tc, x, gn1_g, gn1_b, wq, wk, wv, out_0, out_1, ou
         def gain_and_shift(b, mean, rstd):
             shape = [P, BLOCKS, 2]
             nc.vector.tensor_tensor(
-                out=gain[:, b], in0=affine[:, 0], in1=rstd[:].unsqueeze(2).to_broadcast(shape), op=ALU.mult
+                out=gain[b][:], in0=affine[:, 0], in1=rstd[:].unsqueeze(2).to_broadcast(shape), op=ALU.mult
             )
             moved = small.tile(shape, F32, name="moved")
             nc.vector.tensor_tensor(
-                out=moved[:], in0=gain[:, b], in1=mean.unsqueeze(2).to_broadcast(shape), op=ALU.mult
+                out=moved[:], in0=gain[b][:], in1=mean.unsqueeze(2).to_broadcast(shape), op=ALU.mult
             )
-            nc.vector.tensor_tensor(out=shift[:, b], in0=affine[:, 1], in1=moved[:], op=ALU.subtract)
+            nc.vector.tensor_tensor(out=shift[b][:], in0=affine[:, 1], in1=moved[:], op=ALU.subtract)
 
         def normalise(engine, b, a):
-            pairs = x_words[:, b, a, :].bitcast(BF16).rearrange("p (s e) -> p s e", e=2)
+            pairs = x_words[b][:, :, a, :].bitcast(BF16).rearrange("p j (s e) -> p j s e", e=2)
             for e in range(2):
                 engine.tensor_scalar(
-                    out=h_planes[:, b, a // 2, 2 * (a % 2) + e, :],
-                    in0=pairs[:, :, e],
-                    scalar1=gain[:, b, a, e : e + 1],
-                    scalar2=shift[:, b, a, e : e + 1],
+                    out=h_planes[b, a // 2][:, 2 * (a % 2) + e, :].rearrange("p (j s) -> p j s", j=POS_TILES),
+                    in0=pairs[:, :, :, e],
+                    scalar1=gain[b][:, a, e : e + 1],
+                    scalar2=shift[b][:, a, e : e + 1],
                     op0=ALU.mult,
                     op1=ALU.add,
                 )
@@ -150,22 +157,20 @@ def tile_retnetblock_pa_kernel(tc, x, gn1_g, gn1_b, wq, wk, wv, out_0, out_1, ou
             grouped = h_stage.tile([P, SEQ, PACK], BF16, name="h_grouped", align_bytes=64)
             nc.vector.tensor_copy(
                 out=grouped[:].rearrange("p (n i) t -> p n t i", i=4),
-                in_=h_planes[:, b, c].rearrange("p t (n i) -> p n t i", i=4),
+                in_=h_planes[b, c][:].rearrange("p t (n i) -> p n t i", i=4),
             )
             return grouped
 
         def quantise_h(b, c, grouped):
             nc.vector.quantize_mx(
-                out=h_codes[:, b, c, :].bitcast(FP8X4),
-                scales=h_scales[:, b, c, :],
+                out=h_codes[b, c][:].bitcast(FP8X4),
+                scales=h_scales[b, c][:],
                 in_=grouped[:].rearrange("p s t -> p (s t)"),
             )
 
         def quantise_w(w, quarter, grouped):
-            half, c = quarter // PASSES, quarter % PASSES
-            cols = slice(BANK * half, BANK * half + BANK)
             nc.vector.quantize_mx(
-                out=w_codes[:, w, c, cols].bitcast(FP8X4), scales=w_scales[:, w, c, cols], in_=grouped[:]
+                out=w_codes[w, quarter][:].bitcast(FP8X4), scales=w_scales[w, quarter][:], in_=grouped[:]
             )
 
         tiles = [(w, 0, j) for w in (0, 2, 1) for j in range(POS_TILES)]
@@ -174,18 +179,17 @@ def tile_retnetblock_pa_kernel(tc, x, gn1_g, gn1_b, wq, wk, wv, out_0, out_1, ou
 
         def start_tile(n, pool):
             w, b, j = tiles[n]
-            acc = pool.tile([P, HALVES, BANK], F32, name="acc")
+            acc = [pool.tile([P, BANK], F32, name="acc") for half in range(HALVES)]
             accs.append(acc)
             slots = slice(P * j, P * j + P)
             for half in range(HALVES):
-                cols = slice(BANK * half, BANK * half + BANK)
                 for c in range(PASSES):
                     nc.tensor.matmul_mx(
-                        out=acc[:, half, :],
-                        lhsT=h_codes[:, b, c, slots].bitcast(FP8X4),
-                        lhsT_scale=h_scales[:, b, c, slots],
-                        rhs=w_codes[:, w, c, cols].bitcast(FP8X4),
-                        rhs_scale=w_scales[:, w, c, cols],
+                        out=acc[half][:],
+                        lhsT=h_codes[b, c][:, slots].bitcast(FP8X4),
+                        lhsT_scale=h_scales[b, c][:, slots],
+                        rhs=w_codes[w, PASSES * half + c][:].bitcast(FP8X4),
+                        rhs_scale=w_scales[w, PASSES * half + c][:],
                         start=(c == 0),
                         stop=(c == PASSES - 1),
                     )
@@ -195,7 +199,7 @@ def tile_retnetblock_pa_kernel(tc, x, gn1_g, gn1_b, wq, wk, wv, out_0, out_1, ou
                     squares = scrap.tile([P, BANK], BF16, name="squares")
                     nc.scalar.activation(
                         out=squares[:],
-                        in_=acc[:, half, :],
+                        in_=acc[half][:],
                         func=ACT.Square,
                         accum_out=square_sums[n][:, half : half + 1],
                     )
@@ -219,15 +223,15 @@ def tile_retnetblock_pa_kernel(tc, x, gn1_g, gn1_b, wq, wk, wv, out_0, out_1, ou
             if w < 2:
                 nc.vector.tensor_scalar(
                     out=results[n][:, half, :],
-                    in0=accs[n][:, half, :],
+                    in0=accs[n][half][:],
                     scalar1=inverses[n][:, 0:1],
                     scalar2=None,
                     op0=ALU.mult,
                 )
             elif half == 0 or b == 0:
-                nc.scalar.copy(out=results[n][:, half, :], in_=accs[n][:, half, :])
+                nc.scalar.copy(out=results[n][:, half, :], in_=accs[n][half][:])
             else:
-                nc.vector.tensor_copy(out=results[n][:, half, :], in_=accs[n][:, half, :])
+                nc.vector.tensor_copy(out=results[n][:, half, :], in_=accs[n][half][:])
 
         def store(n):
             w, b, j = tiles[n]
@@ -239,14 +243,11 @@ def tile_retnetblock_pa_kernel(tc, x, gn1_g, gn1_b, wq, wk, wv, out_0, out_1, ou
 
             def x_to_words(b, j):
                 x_t = flip.tile([P, BANK], F32, name="x_t", tag="flip")
-                words = x_sb[:, b, j, :].bitcast(F32)
+                words = x_sb[b][:, j, :].bitcast(F32)
                 for a in range(BLOCKS):
                     cols = slice(P * a, P * a + P)
                     nc.tensor.transpose(x_t[:, cols], words[:, cols], ident[:])
-                nc.scalar.copy(
-                    out=x_words[:, b, :, P * j : P * j + P],
-                    in_=x_t[:].rearrange("p (a s) -> p a s", a=BLOCKS),
-                )
+                nc.scalar.copy(out=x_words[b][:, j].rearrange("p a s -> p (a s)"), in_=x_t[:])
 
             def flip_w(w, quarter):
                 half, c = quarter // PASSES, quarter % PASSES
@@ -319,7 +320,7 @@ def tile_retnetblock_pa_kernel(tc, x, gn1_g, gn1_b, wq, wk, wv, out_0, out_1, ou
             quantise_w(2, 2, staged[2, 2])
             quantise_w(2, 3, staged[2, 3])
             gain_and_shift(1, mean, rstd)
-        sums_high = ctx.enter_context(tc.psum_pool(name="sums_high", bufs=2, reuse_waits="tile"))
+        sums_high = ctx.enter_context(tc.psum_pool(name="sums_high", bufs=4, reuse_waits="tile"))
 
         def advance(n):
             if n < len(tiles):

@@ -17,9 +17,9 @@ PACK = 4
 PASSES = CHAN // (P * PACK)
 BLOCKS = CHAN // (2 * P)
 POS_TILES = SEQ // P
-ROW_TILES = OUTS // P
 BANK = 512
 HALVES = OUTS // BANK
+ROWS = BANK // P
 QUAD = 32
 EPS_GN = 1e-5
 EPS_L2 = 1e-12
@@ -37,7 +37,7 @@ def tile_retnetblock_pa_kernel(tc, x, gn1_g, gn1_b, wq, wk, wv, out_0, out_1, ou
         keep = ctx.enter_context(tc.tile_pool(name="keep", bufs=1))
         small = ctx.enter_context(tc.tile_pool(name="small", bufs=6))
         h_stage = ctx.enter_context(tc.tile_pool(name="h_stage", bufs=2))
-        w_raw = ctx.enter_context(tc.tile_pool(name="w_raw", bufs=2))
+        w_raw = ctx.enter_context(tc.tile_pool(name="w_raw", bufs=4))
         w_stage = ctx.enter_context(tc.tile_pool(name="w_stage", bufs=8))
         out_stage = ctx.enter_context(tc.tile_pool(name="out_stage", bufs=6))
         scrap = ctx.enter_context(tc.tile_pool(name="scrap", bufs=4))
@@ -72,14 +72,13 @@ def tile_retnetblock_pa_kernel(tc, x, gn1_g, gn1_b, wq, wk, wv, out_0, out_1, ou
         nc.vector.memset(affine_rows[:], 0.0)
         nc.sync.dma_start(out=affine_rows[0:BLOCKS, :], in_=gn1_g.rearrange("(a c) -> a c", a=BLOCKS))
         nc.sync.dma_start(out=affine_rows[BLOCKS : 2 * BLOCKS, :], in_=gn1_b.rearrange("(a c) -> a c", a=BLOCKS))
-        w_sb = []
+        w_sb = {}
 
         def load_w(w):
-            w_sb.append(w_raw.tile([P, ROW_TILES, CHAN], BF16, name="w_sb"))
-            w_rows = weights[w].rearrange("(r p) k -> p r k", p=P)
+            w_rows = weights[w].rearrange("(h p i) k -> h p i k", h=HALVES, i=ROWS)
             for half in range(HALVES):
-                rs = slice(4 * half, 4 * half + 4)
-                nc.sync.dma_start(out=w_sb[w][:, rs, :], in_=w_rows[:, rs, :])
+                w_sb[w, half] = w_raw.tile([P, ROWS, CHAN], BF16, name="w_sb")
+                nc.sync.dma_start(out=w_sb[w, half][:], in_=w_rows[half])
 
         load_w(0)
         load_w(1)
@@ -220,18 +219,16 @@ def tile_retnetblock_pa_kernel(tc, x, gn1_g, gn1_b, wq, wk, wv, out_0, out_1, ou
             w, b, j = tiles[n]
             if half == 0:
                 results.append(out_stage.tile([P, HALVES, BANK], F32, name="result"))
+            in_order = accs[n][half][:].rearrange("t (i p) -> t p i", i=ROWS)
+            result = results[n][:, half, :].rearrange("t (p i) -> t p i", i=ROWS)
             if w < 2:
                 nc.vector.tensor_scalar(
-                    out=results[n][:, half, :],
-                    in0=accs[n][half][:],
-                    scalar1=inverses[n][:, 0:1],
-                    scalar2=None,
-                    op0=ALU.mult,
+                    out=result, in0=in_order, scalar1=inverses[n][:, 0:1], scalar2=None, op0=ALU.mult
                 )
             elif half == 0 or b == 0:
-                nc.scalar.copy(out=results[n][:, half, :], in_=accs[n][half][:])
+                nc.scalar.copy(out=result, in_=in_order)
             else:
-                nc.vector.tensor_copy(out=results[n][:, half, :], in_=accs[n][half][:])
+                nc.vector.tensor_copy(out=result, in_=in_order)
 
         def store(n):
             w, b, j = tiles[n]
@@ -257,7 +254,7 @@ def tile_retnetblock_pa_kernel(tc, x, gn1_g, gn1_b, wq, wk, wv, out_0, out_1, ou
                     w_t = flip.tile([P, BANK], F32, name="w_t", tag="flip")
                     for u in range(2):
                         for i in range(2):
-                            words = w_sb[w][:, 4 * half + 2 * pair + i, :].bitcast(F32)
+                            words = w_sb[w, half][:, 2 * pair + i, :].bitcast(F32)
                             a = 2 * c + u
                             nc.tensor.transpose(
                                 w_t[:, 256 * u + P * i : 256 * u + P * i + P],

@@ -13,14 +13,21 @@ ALU = mybir.AluOpType
 
 P = 128
 BATCH, SEQ, CHAN, OUTS = 2, 512, 1024, 1024
+Q, K, V = 0, 1, 2
 PACK = 4
 PASSES = CHAN // (P * PACK)
 BLOCKS = CHAN // (2 * P)
 POS_TILES = SEQ // P
+CHUNKS = 2
+CHUNK_TILES = POS_TILES // CHUNKS
+STATS = 6
 BANK = 512
 HALVES = OUTS // BANK
 ROWS = BANK // P
+QUARTERS = HALVES * PASSES
+BANK_ROWS = BANK // (2 * P)
 QUAD = 32
+RUN = 4
 EPS_GN = 1e-5
 EPS_L2 = 1e-12
 
@@ -36,9 +43,9 @@ def tile_retnetblock_pa_kernel(tc, x, gn1_g, gn1_b, wq, wk, wv, out_0, out_1, ou
         const = ctx.enter_context(tc.tile_pool(name="const", bufs=1))
         keep = ctx.enter_context(tc.tile_pool(name="keep", bufs=1))
         small = ctx.enter_context(tc.tile_pool(name="small", bufs=6))
-        h_stage = ctx.enter_context(tc.tile_pool(name="h_stage", bufs=2))
-        w_raw = ctx.enter_context(tc.tile_pool(name="w_raw", bufs=4))
-        w_stage = ctx.enter_context(tc.tile_pool(name="w_stage", bufs=8))
+        h_stage = ctx.enter_context(tc.tile_pool(name="h_stage", bufs=PASSES))
+        w_raw = ctx.enter_context(tc.tile_pool(name="w_raw", bufs=2 * HALVES))
+        w_stage = ctx.enter_context(tc.tile_pool(name="w_stage", bufs=2 * QUARTERS))
         out_stage = ctx.enter_context(tc.tile_pool(name="out_stage", bufs=6))
         scrap = ctx.enter_context(tc.tile_pool(name="scrap", bufs=4))
         sums_low = ctx.enter_context(tc.psum_pool(name="sums_low", bufs=4))
@@ -47,7 +54,7 @@ def tile_retnetblock_pa_kernel(tc, x, gn1_g, gn1_b, wq, wk, wv, out_0, out_1, ou
         batches = range(BATCH)
         x_sb = [keep.tile([P, POS_TILES, CHAN], BF16, name="x_sb%d" % b) for b in batches]
         x_words = [keep.tile([P, POS_TILES, BLOCKS, P], F32, name="x_words%d" % b) for b in batches]
-        chunk_stats = [keep.tile([P, BLOCKS, 2, 6], F32, name="chunk_stats%d" % b) for b in batches]
+        chunk_stats = [keep.tile([P, BLOCKS, CHUNKS, STATS], F32, name="chunk_stats%d" % b) for b in batches]
         moments = [keep.tile([P, BLOCKS, 2], F32, name="moments%d" % b) for b in batches]
         gain = [keep.tile([P, BLOCKS, 2], F32, name="gain%d" % b) for b in batches]
         shift = [keep.tile([P, BLOCKS, 2], F32, name="shift%d" % b) for b in batches]
@@ -58,15 +65,15 @@ def tile_retnetblock_pa_kernel(tc, x, gn1_g, gn1_b, wq, wk, wv, out_0, out_1, ou
                 h_codes[b, c] = keep.tile([P, SEQ], U32, name="h_codes%d%d" % (b, c), align_bytes=64)
                 h_scales[b, c] = keep.tile([P, SEQ], U8, name="h_scales%d%d" % (b, c), align_bytes=64)
         w_codes, w_scales = {}, {}
-        for w in range(3):
-            for quarter in range(4):
+        for w in (Q, K, V):
+            for quarter in range(QUARTERS):
                 w_codes[w, quarter] = keep.tile([P, BANK], U32, name="w_codes%d%d" % (w, quarter), align_bytes=64)
                 w_scales[w, quarter] = keep.tile([P, BANK], U8, name="w_scales%d%d" % (w, quarter), align_bytes=64)
 
-        for b in range(BATCH):
+        for b in batches:
             x_rows = x[b].rearrange("(p j) c -> p j c", j=POS_TILES)
-            for half in range(2):
-                js = slice(2 * half, 2 * half + 2)
+            for chunk in range(CHUNKS):
+                js = slice(CHUNK_TILES * chunk, CHUNK_TILES * (chunk + 1))
                 nc.sync.dma_start(out=x_sb[b][:, js, :], in_=x_rows[:, js, :])
         affine_rows = const.tile([P, 2 * P], BF16)
         nc.vector.memset(affine_rows[:], 0.0)
@@ -80,15 +87,15 @@ def tile_retnetblock_pa_kernel(tc, x, gn1_g, gn1_b, wq, wk, wv, out_0, out_1, ou
                 w_sb[w, half] = w_raw.tile([P, ROWS, CHAN], BF16, name="w_sb")
                 nc.sync.dma_start(out=w_sb[w, half][:], in_=w_rows[half])
 
-        load_w(0)
-        load_w(1)
+        load_w(Q)
+        load_w(K)
 
         ident = const.tile([P, P], F32)
         make_identity(nc, ident[:])
         group_avg = const.tile([P, P], F32)
         nc.vector.memset(group_avg[:], 0.0)
-        for q in range(P // QUAD):
-            span = slice(QUAD * q, QUAD * q + QUAD)
+        for quad in range(P // QUAD):
+            span = slice(QUAD * quad, QUAD * (quad + 1))
             nc.vector.memset(group_avg[span, span], 1.0 / QUAD)
         eps_gn = const.tile([P, 1], F32)
         nc.vector.memset(eps_gn[:], EPS_GN)
@@ -96,35 +103,30 @@ def tile_retnetblock_pa_kernel(tc, x, gn1_g, gn1_b, wq, wk, wv, out_0, out_1, ou
         nc.scalar.activation(out=warm[:], in_=eps_gn[:], func=ACT.Abs_reciprocal_sqrt)
         affine = const.tile([P, 2, BLOCKS, 2], F32)
 
-        def chunk_statistics(b, half):
+        def chunk_statistics(b, chunk):
+            js = slice(CHUNK_TILES * chunk, CHUNK_TILES * (chunk + 1))
             for a in range(BLOCKS):
-                nc.vector.bn_stats(
-                    out=chunk_stats[b][:, a, half, :],
-                    in_=x_words[b][:, 2 * half : 2 * half + 2, a, :].bitcast(BF16),
-                )
+                nc.vector.bn_stats(out=chunk_stats[b][:, a, chunk, :], in_=x_words[b][:, js, a, :].bitcast(BF16))
 
         def partition_moments(b):
             for a in range(BLOCKS):
-                nc.vector.bn_aggr(
-                    out=moments[b][:, a, :],
-                    in_=chunk_stats[b][:, a, :, :].rearrange("p h s -> p (h s)"),
-                )
-            sq = small.tile([P, BLOCKS], F32, name="sq")
-            nc.vector.tensor_tensor(out=sq[:], in0=moments[b][:, :, 0], in1=moments[b][:, :, 0], op=ALU.mult)
-            nc.vector.tensor_tensor(out=moments[b][:, :, 1], in0=moments[b][:, :, 1], in1=sq[:], op=ALU.add)
+                nc.vector.bn_aggr(out=moments[b][:, a, :], in_=chunk_stats[b][:, a].rearrange("p n m -> p (n m)"))
+            squared = small.tile([P, BLOCKS], F32, name="squared")
+            nc.vector.tensor_tensor(out=squared[:], in0=moments[b][:, :, 0], in1=moments[b][:, :, 0], op=ALU.mult)
+            nc.vector.tensor_tensor(out=moments[b][:, :, 1], in0=moments[b][:, :, 1], in1=squared[:], op=ALU.add)
 
-        def group_moments(b, bank):
+        def group_moments(b, columns):
             nc.tensor.matmul(
-                out=bank, lhsT=group_avg[:], rhs=moments[b][:].rearrange("p a s -> p (a s)"), start=True, stop=True
+                out=columns, lhsT=group_avg[:], rhs=moments[b][:].rearrange("p a m -> p (a m)"), start=True, stop=True
             )
-            both = bank.rearrange("p (a s) -> p a s", s=2)
-            mean_sq = small.tile([P, BLOCKS], F32, name="mean_sq")
-            nc.scalar.activation(out=mean_sq[:], in_=both[:, :, 0], func=ACT.Square)
-            return both[:, :, 0], both[:, :, 1], mean_sq
+            both = columns.rearrange("p (a m) -> p a m", m=2)
+            squared_mean = small.tile([P, BLOCKS], F32, name="squared_mean")
+            nc.scalar.activation(out=squared_mean[:], in_=both[:, :, 0], func=ACT.Square)
+            return both[:, :, 0], both[:, :, 1], squared_mean
 
-        def group_rstd(square_mean, mean_sq):
+        def group_rstd(mean_of_squares, squared_mean):
             var = small.tile([P, BLOCKS], F32, name="var")
-            nc.vector.tensor_tensor(out=var[:], in0=square_mean, in1=mean_sq[:], op=ALU.subtract)
+            nc.vector.tensor_tensor(out=var[:], in0=mean_of_squares, in1=squared_mean[:], op=ALU.subtract)
             rstd = small.tile([P, BLOCKS], F32, name="rstd")
             nc.scalar.activation(out=rstd[:], in_=var[:], func=ACT.Abs_reciprocal_sqrt, bias=eps_gn[:, 0:1])
             return rstd
@@ -141,11 +143,11 @@ def tile_retnetblock_pa_kernel(tc, x, gn1_g, gn1_b, wq, wk, wv, out_0, out_1, ou
             nc.vector.tensor_tensor(out=shift[b][:], in0=affine[:, 1], in1=moved[:], op=ALU.subtract)
 
         def normalise(engine, b, a):
-            pairs = x_words[b][:, :, a, :].bitcast(BF16).rearrange("p j (s e) -> p j s e", e=2)
+            channels = x_words[b][:, :, a, :].bitcast(BF16).rearrange("p j (s e) -> p j s e", e=2)
             for e in range(2):
                 engine.tensor_scalar(
                     out=h_planes[b, a // 2][:, 2 * (a % 2) + e, :].rearrange("p (j s) -> p j s", j=POS_TILES),
-                    in0=pairs[:, :, :, e],
+                    in0=channels[:, :, :, e],
                     scalar1=gain[b][:, a, e : e + 1],
                     scalar2=shift[b][:, a, e : e + 1],
                     op0=ALU.mult,
@@ -155,8 +157,8 @@ def tile_retnetblock_pa_kernel(tc, x, gn1_g, gn1_b, wq, wk, wv, out_0, out_1, ou
         def regroup_h(b, c):
             grouped = h_stage.tile([P, SEQ, PACK], BF16, name="h_grouped", align_bytes=64)
             nc.vector.tensor_copy(
-                out=grouped[:].rearrange("p (n i) t -> p n t i", i=4),
-                in_=h_planes[b, c][:].rearrange("p t (n i) -> p n t i", i=4),
+                out=grouped[:].rearrange("p (g r) t -> p g t r", r=RUN),
+                in_=h_planes[b, c][:].rearrange("p t (g r) -> p g t r", r=RUN),
             )
             return grouped
 
@@ -167,33 +169,37 @@ def tile_retnetblock_pa_kernel(tc, x, gn1_g, gn1_b, wq, wk, wv, out_0, out_1, ou
                 in_=grouped[:].rearrange("p s t -> p (s t)"),
             )
 
-        def quantise_w(w, quarter, grouped):
+        w_grouped = {}
+
+        def quantise_w(w, quarter):
             nc.vector.quantize_mx(
-                out=w_codes[w, quarter][:].bitcast(FP8X4), scales=w_scales[w, quarter][:], in_=grouped[:]
+                out=w_codes[w, quarter][:].bitcast(FP8X4),
+                scales=w_scales[w, quarter][:],
+                in_=w_grouped[w, quarter][:],
             )
 
-        tiles = [(w, 0, j) for w in (0, 2, 1) for j in range(POS_TILES)]
-        tiles.extend([(w, 1, j) for j in range(POS_TILES) for w in (0, 1, 2)])
+        tiles = [(w, 0, j) for w in (Q, V, K) for j in range(POS_TILES)]
+        tiles.extend([(w, 1, j) for j in range(POS_TILES) for w in (Q, K, V)])
         accs, square_sums, inverses, results = [], [], [], []
 
         def start_tile(n, pool):
             w, b, j = tiles[n]
             acc = [pool.tile([P, BANK], F32, name="acc") for half in range(HALVES)]
             accs.append(acc)
-            slots = slice(P * j, P * j + P)
+            positions = slice(P * j, P * (j + 1))
             for half in range(HALVES):
                 for c in range(PASSES):
                     nc.tensor.matmul_mx(
                         out=acc[half][:],
-                        lhsT=h_codes[b, c][:, slots].bitcast(FP8X4),
-                        lhsT_scale=h_scales[b, c][:, slots],
+                        lhsT=h_codes[b, c][:, positions].bitcast(FP8X4),
+                        lhsT_scale=h_scales[b, c][:, positions],
                         rhs=w_codes[w, PASSES * half + c][:].bitcast(FP8X4),
                         rhs_scale=w_scales[w, PASSES * half + c][:],
                         start=(c == 0),
                         stop=(c == PASSES - 1),
                     )
-            square_sums.append(small.tile([P, HALVES], F32, name="square_sums") if w < 2 else None)
-            if w < 2:
+            square_sums.append(small.tile([P, HALVES], F32, name="square_sums") if w != V else None)
+            if w != V:
                 for half in range(HALVES):
                     squares = scrap.tile([P, BANK], BF16, name="squares")
                     nc.scalar.activation(
@@ -204,24 +210,24 @@ def tile_retnetblock_pa_kernel(tc, x, gn1_g, gn1_b, wq, wk, wv, out_0, out_1, ou
                     )
 
         def inverse_norm(n):
-            inverses.append(small.tile([P, 1], F32, name="inverse") if tiles[n][0] < 2 else None)
-            if tiles[n][0] < 2:
-                raw = small.tile([P, 1], F32, name="raw")
+            inverses.append(small.tile([P, 1], F32, name="inverse") if tiles[n][0] != V else None)
+            if tiles[n][0] != V:
+                unclamped = small.tile([P, 1], F32, name="unclamped")
                 nc.scalar.activation(
-                    out=raw[:],
+                    out=unclamped[:],
                     in_=square_sums[n][:, 0:1],
                     func=ACT.Abs_reciprocal_sqrt,
                     bias=square_sums[n][:, 1:2],
                 )
-                nc.vector.tensor_scalar_min(out=inverses[n][:], in0=raw[:], scalar1=1.0 / EPS_L2)
+                nc.vector.tensor_scalar_min(out=inverses[n][:], in0=unclamped[:], scalar1=1.0 / EPS_L2)
 
         def leave_psum(n, half):
             w, b, j = tiles[n]
             if half == 0:
                 results.append(out_stage.tile([P, HALVES, BANK], F32, name="result"))
-            in_order = accs[n][half][:].rearrange("t (i p) -> t p i", i=ROWS)
-            result = results[n][:, half, :].rearrange("t (p i) -> t p i", i=ROWS)
-            if w < 2:
+            in_order = accs[n][half][:].rearrange("s (i p) -> s p i", i=ROWS)
+            result = results[n][:, half, :].rearrange("s (p i) -> s p i", i=ROWS)
+            if w != V:
                 nc.vector.tensor_scalar(
                     out=result, in0=in_order, scalar1=inverses[n][:, 0:1], scalar2=None, op0=ALU.mult
                 )
@@ -235,65 +241,65 @@ def tile_retnetblock_pa_kernel(tc, x, gn1_g, gn1_b, wq, wk, wv, out_0, out_1, ou
             out_rows = outs[w][b].rearrange("(p j) o -> j p o", j=POS_TILES)
             nc.sync.dma_start(out=out_rows[j], in_=results[n][:].rearrange("p h o -> p (h o)"))
 
-        staged = {}
-        with tc.psum_pool(name="flip", bufs=4) as flip:
+        with tc.psum_pool(name="turned", bufs=4) as turned:
 
-            def x_to_words(b, j):
-                x_t = flip.tile([P, BANK], F32, name="x_t", tag="flip")
+            def transpose_x(b, j):
+                x_t = turned.tile([P, BANK], F32, name="x_t", tag="turned")
                 words = x_sb[b][:, j, :].bitcast(F32)
                 for a in range(BLOCKS):
-                    cols = slice(P * a, P * a + P)
+                    cols = slice(P * a, P * (a + 1))
                     nc.tensor.transpose(x_t[:, cols], words[:, cols], ident[:])
                 nc.scalar.copy(out=x_words[b][:, j].rearrange("p a s -> p (a s)"), in_=x_t[:])
 
-            def flip_w(w, quarter):
+            def transpose_w(w, quarter):
                 half, c = quarter // PASSES, quarter % PASSES
                 grouped = w_stage.tile([P, BANK * PACK], BF16, name="w_grouped", align_bytes=64)
                 grouped_words = grouped[:].bitcast(F32).rearrange("p (o u) -> p o u", u=2)
-                for pair in range(2):
-                    w_t = flip.tile([P, BANK], F32, name="w_t", tag="flip")
+                width = BANK_ROWS * P
+                for bank in range(ROWS // BANK_ROWS):
+                    w_t = turned.tile([P, BANK], F32, name="w_t", tag="turned")
                     for u in range(2):
-                        for i in range(2):
-                            words = w_sb[w, half][:, 2 * pair + i, :].bitcast(F32)
+                        for r in range(BANK_ROWS):
+                            words = w_sb[w, half][:, BANK_ROWS * bank + r, :].bitcast(F32)
                             a = 2 * c + u
                             nc.tensor.transpose(
-                                w_t[:, 256 * u + P * i : 256 * u + P * i + P],
-                                words[:, P * a : P * a + P],
+                                w_t[:, width * u + P * r : width * u + P * (r + 1)],
+                                words[:, P * a : P * (a + 1)],
                                 ident[:],
                             )
                     nc.scalar.copy(
-                        out=grouped_words[:, 256 * pair : 256 * pair + 256, :],
+                        out=grouped_words[:, width * bank : width * (bank + 1), :],
                         in_=w_t[:].rearrange("p (u o) -> p o u", u=2),
                     )
-                staged[w, quarter] = grouped
+                w_grouped[w, quarter] = grouped
 
             for j in range(POS_TILES):
-                x_to_words(0, j)
-                if j % 2 == 1:
-                    chunk_statistics(0, j // 2)
+                transpose_x(0, j)
+                if j % CHUNK_TILES == CHUNK_TILES - 1:
+                    chunk_statistics(0, j // CHUNK_TILES)
             for j in range(POS_TILES):
-                x_to_words(1, j)
-            affine_t = flip.tile([P, BANK], F32, name="affine_t", tag="flip")
+                transpose_x(1, j)
+            affine_t = turned.tile([P, BANK], F32, name="affine_t", tag="turned")
             nc.tensor.transpose(affine_t[:, 0:P], affine_rows[:].bitcast(F32), ident[:])
             nc.vector.tensor_copy(
-                out=affine[:].rearrange("p s a e -> p (s a e)"),
+                out=affine[:].rearrange("p v a e -> p (v a e)"),
                 in_=affine_t[:, 0 : 2 * BLOCKS].bitcast(BF16),
             )
             partition_moments(0)
-            flip_w(0, 0)
-            flip_w(0, 1)
-            group_t = flip.tile([P, BANK], F32, name="group_t", tag="flip")
-            mean, square_mean, mean_sq = group_moments(0, group_t[:, 0 : 2 * BLOCKS])
-            flip_w(0, 2)
+            transpose_w(Q, 0)
+            transpose_w(Q, 1)
+            group_t = turned.tile([P, BANK], F32, name="group_t", tag="turned")
+            mean, mean_of_squares, squared_mean = group_moments(0, group_t[:, 0 : 2 * BLOCKS])
+            transpose_w(Q, 2)
             chunk_statistics(1, 0)
-            rstd = group_rstd(square_mean, mean_sq)
-            flip_w(0, 3)
-            load_w(2)
-            quantise_w(0, 0, staged[0, 0])
-            quantise_w(0, 1, staged[0, 1])
+            rstd = group_rstd(mean_of_squares, squared_mean)
+            transpose_w(Q, 3)
+            load_w(V)
+            quantise_w(Q, 0)
+            quantise_w(Q, 1)
             gain_and_shift(0, mean, rstd)
-            for quarter in range(4):
-                flip_w(1, quarter)
+            for quarter in range(QUARTERS):
+                transpose_w(K, quarter)
             normalise(nc.vector, 0, 0)
             normalise(nc.vector, 0, 1)
             grouped_0 = regroup_h(0, 0)
@@ -301,21 +307,21 @@ def tile_retnetblock_pa_kernel(tc, x, gn1_g, gn1_b, wq, wk, wv, out_0, out_1, ou
             normalise(nc.vector, 0, 3)
             quantise_h(0, 0, grouped_0)
             grouped_1 = regroup_h(0, 1)
-            quantise_w(0, 2, staged[0, 2])
+            quantise_w(Q, 2)
             quantise_h(0, 1, grouped_1)
-            quantise_w(0, 3, staged[0, 3])
-            for quarter in range(4):
-                flip_w(2, quarter)
+            quantise_w(Q, 3)
+            for quarter in range(QUARTERS):
+                transpose_w(V, quarter)
             chunk_statistics(1, 1)
             partition_moments(1)
             start_tile(0, sums_low)
-            group_t = flip.tile([P, BANK], F32, name="group_t", tag="flip")
-            mean, square_mean, mean_sq = group_moments(1, group_t[:, 0 : 2 * BLOCKS])
-            quantise_w(2, 0, staged[2, 0])
-            quantise_w(2, 1, staged[2, 1])
-            rstd = group_rstd(square_mean, mean_sq)
-            quantise_w(2, 2, staged[2, 2])
-            quantise_w(2, 3, staged[2, 3])
+            group_t = turned.tile([P, BANK], F32, name="group_t", tag="turned")
+            mean, mean_of_squares, squared_mean = group_moments(1, group_t[:, 0 : 2 * BLOCKS])
+            quantise_w(V, 0)
+            quantise_w(V, 1)
+            rstd = group_rstd(mean_of_squares, squared_mean)
+            quantise_w(V, 2)
+            quantise_w(V, 3)
             gain_and_shift(1, mean, rstd)
         sums_high = ctx.enter_context(tc.psum_pool(name="sums_high", bufs=4, reuse_waits="tile"))
 
@@ -332,8 +338,8 @@ def tile_retnetblock_pa_kernel(tc, x, gn1_g, gn1_b, wq, wk, wv, out_0, out_1, ou
         for a in range(BLOCKS):
             advance(1 + a)
             normalise(nc.gpsimd, 1, a)
-        for quarter in range(4):
-            quantise_w(1, quarter, staged[1, quarter])
+        for quarter in range(QUARTERS):
+            quantise_w(K, quarter)
         grouped_0 = regroup_h(1, 0)
         grouped_1 = regroup_h(1, 1)
         quantise_h(1, 0, grouped_0)

@@ -34,6 +34,9 @@ EPS_L2 = 1e-12
 FLOPS = 2 * BATCH * SEQ * CHAN * 3 * OUTS
 
 
+LAG = 2
+
+
 def tile_retnetblock_pa_kernel(tc, x, gn1_g, gn1_b, wq, wk, wv, out_0, out_1, out_2):
     nc = tc.nc
     weights = (wq, wk, wv)
@@ -44,9 +47,9 @@ def tile_retnetblock_pa_kernel(tc, x, gn1_g, gn1_b, wq, wk, wv, out_0, out_1, ou
         keep = ctx.enter_context(tc.tile_pool(name="keep", bufs=1))
         small = ctx.enter_context(tc.tile_pool(name="small", bufs=6))
         h_stage = ctx.enter_context(tc.tile_pool(name="h_stage", bufs=PASSES))
-        w_raw = ctx.enter_context(tc.tile_pool(name="w_raw", bufs=2 * HALVES))
+        w_raw = ctx.enter_context(tc.tile_pool(name="w_raw", bufs=3 * HALVES))
         w_stage = ctx.enter_context(tc.tile_pool(name="w_stage", bufs=2 * QUARTERS))
-        out_stage = ctx.enter_context(tc.tile_pool(name="out_stage", bufs=6))
+        out_stage = ctx.enter_context(tc.tile_pool(name="out_stage", bufs=8))
         scrap = ctx.enter_context(tc.tile_pool(name="scrap", bufs=4))
         sums_low = ctx.enter_context(tc.psum_pool(name="sums_low", bufs=4))
         ctx.enter_context(tc.manual_schedule())
@@ -87,8 +90,8 @@ def tile_retnetblock_pa_kernel(tc, x, gn1_g, gn1_b, wq, wk, wv, out_0, out_1, ou
                 w_sb[w, half] = w_raw.tile([P, ROWS, CHAN], BF16, name="w_sb")
                 nc.sync.dma_start(out=w_sb[w, half][:], in_=w_rows[half])
 
-        load_w(Q)
-        load_w(K)
+        for w in (V, Q, K):
+            load_w(w)
 
         ident = const.tile([P, P], F32)
         make_identity(nc, ident[:])
@@ -178,19 +181,20 @@ def tile_retnetblock_pa_kernel(tc, x, gn1_g, gn1_b, wq, wk, wv, out_0, out_1, ou
                 in_=w_grouped[w, quarter][:],
             )
 
-        tiles = [(w, 0, j) for w in (Q, V, K) for j in range(POS_TILES)]
+        tiles = [(V, 0, j) for j in range(POS_TILES - 1)]
+        tiles.extend([(w, 0, j) for w in (Q, K) for j in range(POS_TILES)])
+        tiles.append((V, 0, POS_TILES - 1))
         tiles.extend([(w, 1, j) for j in range(POS_TILES) for w in (Q, K, V)])
-        accs, square_sums, inverses, results = [], [], [], []
+        accs, square_sums, inverses, results = {}, {}, {}, {}
 
-        def start_tile(n, pool):
+        def multiply(n, pool):
             w, b, j = tiles[n]
-            acc = [pool.tile([P, BANK], F32, name="acc") for half in range(HALVES)]
-            accs.append(acc)
+            accs[n] = [pool.tile([P, BANK], F32, name="acc") for half in range(HALVES)]
             positions = slice(P * j, P * (j + 1))
             for half in range(HALVES):
                 for c in range(PASSES):
                     nc.tensor.matmul_mx(
-                        out=acc[half][:],
+                        out=accs[n][half][:],
                         lhsT=h_codes[b, c][:, positions].bitcast(FP8X4),
                         lhsT_scale=h_scales[b, c][:, positions],
                         rhs=w_codes[w, PASSES * half + c][:].bitcast(FP8X4),
@@ -198,40 +202,58 @@ def tile_retnetblock_pa_kernel(tc, x, gn1_g, gn1_b, wq, wk, wv, out_0, out_1, ou
                         start=(c == 0),
                         stop=(c == PASSES - 1),
                     )
-            square_sums.append(small.tile([P, HALVES], F32, name="square_sums") if w != V else None)
-            if w != V:
-                for half in range(HALVES):
-                    squares = scrap.tile([P, BANK], BF16, name="squares")
-                    nc.scalar.activation(
-                        out=squares[:],
-                        in_=acc[half][:],
-                        func=ACT.Square,
-                        accum_out=square_sums[n][:, half : half + 1],
-                    )
 
-        def inverse_norm(n):
-            inverses.append(small.tile([P, 1], F32, name="inverse") if tiles[n][0] != V else None)
-            if tiles[n][0] != V:
-                unclamped = small.tile([P, 1], F32, name="unclamped")
+        def square(n):
+            if tiles[n][0] == V:
+                return
+            square_sums[n] = small.tile([P, HALVES], F32, name="square_sums")
+            for half in range(HALVES):
+                squares = scrap.tile([P, BANK], BF16, name="squares")
                 nc.scalar.activation(
-                    out=unclamped[:],
-                    in_=square_sums[n][:, 0:1],
-                    func=ACT.Abs_reciprocal_sqrt,
-                    bias=square_sums[n][:, 1:2],
+                    out=squares[:],
+                    in_=accs[n][half][:],
+                    func=ACT.Square,
+                    accum_out=square_sums[n][:, half : half + 1],
                 )
-                nc.vector.tensor_scalar_min(out=inverses[n][:], in0=unclamped[:], scalar1=1.0 / EPS_L2)
 
-        def leave_psum(n, half):
+        unclamped = {}
+
+        def root(n):
+            if tiles[n][0] == V:
+                return
+            unclamped[n] = small.tile([P, 1], F32, name="unclamped")
+            nc.scalar.activation(
+                out=unclamped[n][:],
+                in_=square_sums[n][:, 0:1],
+                func=ACT.Abs_reciprocal_sqrt,
+                bias=square_sums[n][:, 1:2],
+            )
+
+        def clamp(n):
+            if tiles[n][0] == V:
+                return
+            inverses[n] = small.tile([P, 1], F32, name="inverse")
+            nc.vector.tensor_scalar_min(out=inverses[n][:], in0=unclamped[n][:], scalar1=1.0 / EPS_L2)
+
+        def who(n, half):
             w, b, j = tiles[n]
-            if half == 0:
-                results.append(out_stage.tile([P, HALVES, BANK], F32, name="result"))
+            if w == V:
+                return "S" if b == 0 else "SV"[half]
+            return "SV"[half] if (w, b) == (K, 0) and j < CHUNK_TILES else "V"
+
+        def leave_psum(n, half, engine):
+            w, b, j = tiles[n]
+            if n not in results:
+                results[n] = out_stage.tile([P, HALVES, BANK], F32, name="result")
             in_order = accs[n][half][:].rearrange("s (i p) -> s p i", i=ROWS)
             result = results[n][:, half, :].rearrange("s (p i) -> s p i", i=ROWS)
-            if w != V:
+            if w != V and engine == "V":
                 nc.vector.tensor_scalar(
                     out=result, in0=in_order, scalar1=inverses[n][:, 0:1], scalar2=None, op0=ALU.mult
                 )
-            elif half == 0 or b == 0:
+            elif w != V:
+                nc.scalar.activation(out=result, in_=in_order, func=ACT.Copy, scale=inverses[n][:, 0:1])
+            elif engine == "S":
                 nc.scalar.copy(out=result, in_=in_order)
             else:
                 nc.vector.tensor_copy(out=result, in_=in_order)
@@ -240,6 +262,41 @@ def tile_retnetblock_pa_kernel(tc, x, gn1_g, gn1_b, wq, wk, wv, out_0, out_1, ou
             w, b, j = tiles[n]
             out_rows = outs[w][b].rearrange("(p j) o -> j p o", j=POS_TILES)
             nc.sync.dma_start(out=out_rows[j], in_=results[n][:].rearrange("p h o -> p (h o)"))
+
+        pools = [sums_low]
+        grouped_h1 = {}
+        first_h1_job = tiles.index((K, 0, POS_TILES - 1)) - 2 * PASSES
+
+        def step(n):
+            if n < len(tiles):
+                multiply(n, pools[n % len(pools)])
+                square(n)
+                if tiles[n][0] == V:
+                    for half in range(HALVES):
+                        if who(n, half) == "S":
+                            leave_psum(n, half, "S")
+                    if all(who(n, half) == "S" for half in range(HALVES)):
+                        store(n)
+            if 0 <= n - 1 < len(tiles):
+                root(n - 1)
+            if n == tiles.index((Q, 0, 0)):
+                for quarter in range(QUARTERS):
+                    quantise_w(K, quarter)
+            m = n - LAG
+            if 0 <= m - first_h1_job < 2 * PASSES:
+                c, quantise = divmod(m - first_h1_job, 2)
+                if quantise:
+                    quantise_h(1, c, grouped_h1[c])
+                else:
+                    grouped_h1[c] = regroup_h(1, c)
+            if 0 <= m < len(tiles):
+                late = [half for half in range(HALVES) if tiles[m][0] != V or who(m, half) == "V"]
+                for half in late:
+                    leave_psum(m, half, who(m, half))
+                if late:
+                    store(m)
+            if 0 <= m + 1 < len(tiles):
+                clamp(m + 1)
 
         with tc.psum_pool(name="turned", bufs=4) as turned:
 
@@ -286,20 +343,19 @@ def tile_retnetblock_pa_kernel(tc, x, gn1_g, gn1_b, wq, wk, wv, out_0, out_1, ou
                 in_=affine_t[:, 0 : 2 * BLOCKS].bitcast(BF16),
             )
             partition_moments(0)
-            transpose_w(Q, 0)
-            transpose_w(Q, 1)
+            transpose_w(V, 0)
+            transpose_w(V, 1)
             group_t = turned.tile([P, BANK], F32, name="group_t", tag="turned")
             mean, mean_of_squares, squared_mean = group_moments(0, group_t[:, 0 : 2 * BLOCKS])
-            transpose_w(Q, 2)
+            transpose_w(V, 2)
             chunk_statistics(1, 0)
             rstd = group_rstd(mean_of_squares, squared_mean)
-            transpose_w(Q, 3)
-            load_w(V)
-            quantise_w(Q, 0)
-            quantise_w(Q, 1)
+            transpose_w(V, 3)
+            quantise_w(V, 0)
+            quantise_w(V, 1)
             gain_and_shift(0, mean, rstd)
             for quarter in range(QUARTERS):
-                transpose_w(K, quarter)
+                transpose_w(Q, quarter)
             normalise(nc.vector, 0, 0)
             normalise(nc.vector, 0, 1)
             grouped_0 = regroup_h(0, 0)
@@ -307,43 +363,26 @@ def tile_retnetblock_pa_kernel(tc, x, gn1_g, gn1_b, wq, wk, wv, out_0, out_1, ou
             normalise(nc.vector, 0, 3)
             quantise_h(0, 0, grouped_0)
             grouped_1 = regroup_h(0, 1)
-            quantise_w(Q, 2)
+            quantise_w(V, 2)
             quantise_h(0, 1, grouped_1)
-            quantise_w(Q, 3)
+            quantise_w(V, 3)
             for quarter in range(QUARTERS):
-                transpose_w(V, quarter)
+                transpose_w(K, quarter)
             chunk_statistics(1, 1)
             partition_moments(1)
-            start_tile(0, sums_low)
+            step(0)
+            step(1)
             group_t = turned.tile([P, BANK], F32, name="group_t", tag="turned")
             mean, mean_of_squares, squared_mean = group_moments(1, group_t[:, 0 : 2 * BLOCKS])
-            quantise_w(V, 0)
-            quantise_w(V, 1)
+            quantise_w(Q, 0)
+            quantise_w(Q, 1)
+            step(2)
             rstd = group_rstd(mean_of_squares, squared_mean)
-            quantise_w(V, 2)
-            quantise_w(V, 3)
+            quantise_w(Q, 2)
+            quantise_w(Q, 3)
             gain_and_shift(1, mean, rstd)
-        sums_high = ctx.enter_context(tc.psum_pool(name="sums_high", bufs=4, reuse_waits="tile"))
-
-        def advance(n):
-            if n < len(tiles):
-                start_tile(n, (sums_low, sums_high)[n % 2])
-            leave_psum(n - 1, 0)
-            if n < len(tiles):
-                inverse_norm(n)
-            leave_psum(n - 1, 1)
-            store(n - 1)
-
-        inverse_norm(0)
+        pools.append(ctx.enter_context(tc.psum_pool(name="sums_high", bufs=4, reuse_waits="tile")))
         for a in range(BLOCKS):
-            advance(1 + a)
             normalise(nc.gpsimd, 1, a)
-        for quarter in range(QUARTERS):
-            quantise_w(K, quarter)
-        grouped_0 = regroup_h(1, 0)
-        grouped_1 = regroup_h(1, 1)
-        quantise_h(1, 0, grouped_0)
-        quantise_h(1, 1, grouped_1)
-
-        for n in range(1 + BLOCKS, len(tiles) + 1):
-            advance(n)
+        for n in range(3, len(tiles) + LAG):
+            step(n)

@@ -106,16 +106,20 @@ def tile_retnetblock_pa_kernel(tc, x, gn1_g, gn1_b, wq, wk, wv, out_0, out_1, ou
         nc.scalar.activation(out=warm[:], in_=eps_gn[:], func=ACT.Abs_reciprocal_sqrt)
         affine = const.tile([P, 2, BLOCKS, 2], F32)
 
-        def chunk_statistics(b, chunk):
+        def block_statistics(b, chunk, a):
             js = slice(CHUNK_TILES * chunk, CHUNK_TILES * (chunk + 1))
-            for a in range(BLOCKS):
-                nc.vector.bn_stats(out=chunk_stats[b][:, a, chunk, :], in_=x_words[b][:, js, a, :].bitcast(BF16))
+            nc.vector.bn_stats(out=chunk_stats[b][:, a, chunk, :], in_=x_words[b][:, js, a, :].bitcast(BF16))
 
-        def partition_moments(b):
+        def aggregate(b):
             for a in range(BLOCKS):
                 nc.vector.bn_aggr(out=moments[b][:, a, :], in_=chunk_stats[b][:, a].rearrange("p n m -> p (n m)"))
+
+        def square_means(b):
             squared = small.tile([P, BLOCKS], F32, name="squared")
             nc.vector.tensor_tensor(out=squared[:], in0=moments[b][:, :, 0], in1=moments[b][:, :, 0], op=ALU.mult)
+            return squared
+
+        def means_of_squares(b, squared):
             nc.vector.tensor_tensor(out=moments[b][:, :, 1], in0=moments[b][:, :, 1], in1=squared[:], op=ALU.add)
 
         def group_moments(b, columns):
@@ -134,15 +138,21 @@ def tile_retnetblock_pa_kernel(tc, x, gn1_g, gn1_b, wq, wk, wv, out_0, out_1, ou
             nc.scalar.activation(out=rstd[:], in_=var[:], func=ACT.Abs_reciprocal_sqrt, bias=eps_gn[:, 0:1])
             return rstd
 
-        def gain_and_shift(b, mean, rstd):
-            shape = [P, BLOCKS, 2]
+        by_channel = [P, BLOCKS, 2]
+
+        def gains(b, rstd):
             nc.vector.tensor_tensor(
-                out=gain[b][:], in0=affine[:, 0], in1=rstd[:].unsqueeze(2).to_broadcast(shape), op=ALU.mult
+                out=gain[b][:], in0=affine[:, 0], in1=rstd[:].unsqueeze(2).to_broadcast(by_channel), op=ALU.mult
             )
-            moved = small.tile(shape, F32, name="moved")
+
+        def moves(b, mean):
+            moved = small.tile(by_channel, F32, name="moved")
             nc.vector.tensor_tensor(
-                out=moved[:], in0=gain[b][:], in1=mean.unsqueeze(2).to_broadcast(shape), op=ALU.mult
+                out=moved[:], in0=gain[b][:], in1=mean.unsqueeze(2).to_broadcast(by_channel), op=ALU.mult
             )
+            return moved
+
+        def shifts(b, moved):
             nc.vector.tensor_tensor(out=shift[b][:], in0=affine[:, 1], in1=moved[:], op=ALU.subtract)
 
         def normalise(engine, b, a):
@@ -203,18 +213,18 @@ def tile_retnetblock_pa_kernel(tc, x, gn1_g, gn1_b, wq, wk, wv, out_0, out_1, ou
                         stop=(c == PASSES - 1),
                     )
 
-        def square(n):
+        def square(n, half):
             if tiles[n][0] == V:
                 return
-            square_sums[n] = small.tile([P, HALVES], F32, name="square_sums")
-            for half in range(HALVES):
-                squares = scrap.tile([P, BANK], BF16, name="squares")
-                nc.scalar.activation(
-                    out=squares[:],
-                    in_=accs[n][half][:],
-                    func=ACT.Square,
-                    accum_out=square_sums[n][:, half : half + 1],
-                )
+            if half == 0:
+                square_sums[n] = small.tile([P, HALVES], F32, name="square_sums")
+            squares = scrap.tile([P, BANK], BF16, name="squares")
+            nc.scalar.activation(
+                out=squares[:],
+                in_=accs[n][half][:],
+                func=ACT.Square,
+                accum_out=square_sums[n][:, half : half + 1],
+            )
 
         unclamped = {}
 
@@ -270,18 +280,15 @@ def tile_retnetblock_pa_kernel(tc, x, gn1_g, gn1_b, wq, wk, wv, out_0, out_1, ou
         def step(n):
             if n < len(tiles):
                 multiply(n, pools[n % len(pools)])
-                square(n)
-                if tiles[n][0] == V:
-                    for half in range(HALVES):
-                        if who(n, half) == "S":
-                            leave_psum(n, half, "S")
-                    if all(who(n, half) == "S" for half in range(HALVES)):
-                        store(n)
-            if 0 <= n - 1 < len(tiles):
-                root(n - 1)
-            if n == tiles.index((Q, 0, 0)):
-                for quarter in range(QUARTERS):
-                    quantise_w(K, quarter)
+            for half in range(HALVES):
+                if n < len(tiles):
+                    square(n, half)
+                    if tiles[n][0] == V and who(n, half) == "S":
+                        leave_psum(n, half, "S")
+                if half == 0 and 0 <= n - 1 < len(tiles):
+                    root(n - 1)
+            if n < len(tiles) and tiles[n][0] == V and all(who(n, half) == "S" for half in range(HALVES)):
+                store(n)
             m = n - LAG
             if 0 <= m - first_h1_job < 2 * PASSES:
                 c, quantise = divmod(m - first_h1_job, 2)
@@ -291,12 +298,14 @@ def tile_retnetblock_pa_kernel(tc, x, gn1_g, gn1_b, wq, wk, wv, out_0, out_1, ou
                     grouped_h1[c] = regroup_h(1, c)
             if 0 <= m < len(tiles):
                 late = [half for half in range(HALVES) if tiles[m][0] != V or who(m, half) == "V"]
-                for half in late:
+                for half in late[:-1]:
                     leave_psum(m, half, who(m, half))
-                if late:
-                    store(m)
             if 0 <= m + 1 < len(tiles):
                 clamp(m + 1)
+            if 0 <= m < len(tiles):
+                for half in late[-1:]:
+                    leave_psum(m, half, who(m, half))
+                    store(m)
 
         with tc.psum_pool(name="turned", bufs=4) as turned:
 
@@ -333,54 +342,71 @@ def tile_retnetblock_pa_kernel(tc, x, gn1_g, gn1_b, wq, wk, wv, out_0, out_1, ou
             for j in range(POS_TILES):
                 transpose_x(0, j)
                 if j % CHUNK_TILES == CHUNK_TILES - 1:
-                    chunk_statistics(0, j // CHUNK_TILES)
+                    for a in range(BLOCKS):
+                        block_statistics(0, j // CHUNK_TILES, a)
             for j in range(POS_TILES):
                 transpose_x(1, j)
             affine_t = turned.tile([P, BANK], F32, name="affine_t", tag="turned")
             nc.tensor.transpose(affine_t[:, 0:P], affine_rows[:].bitcast(F32), ident[:])
+            aggregate(0)
             nc.vector.tensor_copy(
                 out=affine[:].rearrange("p v a e -> p (v a e)"),
                 in_=affine_t[:, 0 : 2 * BLOCKS].bitcast(BF16),
             )
-            partition_moments(0)
+            squared = square_means(0)
             transpose_w(V, 0)
             transpose_w(V, 1)
+            block_statistics(1, 0, 0)
+            means_of_squares(0, squared)
             group_t = turned.tile([P, BANK], F32, name="group_t", tag="turned")
             mean, mean_of_squares, squared_mean = group_moments(0, group_t[:, 0 : 2 * BLOCKS])
             transpose_w(V, 2)
-            chunk_statistics(1, 0)
+            for a in range(1, BLOCKS):
+                block_statistics(1, 0, a)
             rstd = group_rstd(mean_of_squares, squared_mean)
             transpose_w(V, 3)
             quantise_w(V, 0)
+            gains(0, rstd)
             quantise_w(V, 1)
-            gain_and_shift(0, mean, rstd)
+            moved = moves(0, mean)
+            quantise_w(V, 2)
+            shifts(0, moved)
+            quantise_w(V, 3)
             for quarter in range(QUARTERS):
                 transpose_w(Q, quarter)
             normalise(nc.vector, 0, 0)
             normalise(nc.vector, 0, 1)
-            grouped_0 = regroup_h(0, 0)
             normalise(nc.vector, 0, 2)
+            grouped_0 = regroup_h(0, 0)
             normalise(nc.vector, 0, 3)
             quantise_h(0, 0, grouped_0)
             grouped_1 = regroup_h(0, 1)
-            quantise_w(V, 2)
+            block_statistics(1, 1, 0)
             quantise_h(0, 1, grouped_1)
-            quantise_w(V, 3)
             for quarter in range(QUARTERS):
                 transpose_w(K, quarter)
-            chunk_statistics(1, 1)
-            partition_moments(1)
+            for a in range(1, BLOCKS):
+                block_statistics(1, 1, a)
+            aggregate(1)
             step(0)
             step(1)
+            quantise_w(Q, 0)
+            squared = square_means(1)
+            quantise_w(Q, 1)
+            means_of_squares(1, squared)
             group_t = turned.tile([P, BANK], F32, name="group_t", tag="turned")
             mean, mean_of_squares, squared_mean = group_moments(1, group_t[:, 0 : 2 * BLOCKS])
-            quantise_w(Q, 0)
-            quantise_w(Q, 1)
+            quantise_w(Q, 2)
             step(2)
             rstd = group_rstd(mean_of_squares, squared_mean)
-            quantise_w(Q, 2)
             quantise_w(Q, 3)
-            gain_and_shift(1, mean, rstd)
+            quantise_w(K, 0)
+            gains(1, rstd)
+            quantise_w(K, 1)
+            moved = moves(1, mean)
+            quantise_w(K, 2)
+            shifts(1, moved)
+            quantise_w(K, 3)
         pools.append(ctx.enter_context(tc.psum_pool(name="sums_high", bufs=4, reuse_waits="tile")))
         for a in range(BLOCKS):
             normalise(nc.gpsimd, 1, a)

from contextlib import ExitStack

import concourse.mybir as mybir
from concourse.masks import make_identity

F32 = mybir.dt.float32
BF16 = mybir.dt.bfloat16
U32 = mybir.dt.uint32
U8 = mybir.dt.uint8
FP8X4 = mybir.dt.float8_e4m3fn_x4
ACT = mybir.ActivationFunctionType
ALU = mybir.AluOpType

P = 128
BATCH, SEQ, CHAN, OUTS = 2, 512, 1024, 1024
Q, K, V = 0, 1, 2
PACK = 4
PASSES = CHAN // (P * PACK)
BLOCKS = CHAN // (2 * P)
POS_TILES = SEQ // P
CHUNKS = 2
CHUNK_TILES = POS_TILES // CHUNKS
STATS = 6
BANK = 512
HALVES = OUTS // BANK
ROWS = BANK // P
QUARTERS = HALVES * PASSES
BANK_ROWS = BANK // (2 * P)
QUAD = 32
RUN = 4
EPS_GN = 1e-5
EPS_L2 = 1e-12

FLOPS = 2 * BATCH * SEQ * CHAN * 3 * OUTS


LAG = 2


def tile_retnetblock_pa_kernel(tc, x, gn1_g, gn1_b, wq, wk, wv, out_0, out_1, out_2):
    nc = tc.nc
    weights = (wq, wk, wv)
    outs = (out_0, out_1, out_2)

    with ExitStack() as ctx:
        const = ctx.enter_context(tc.tile_pool(name="const", bufs=1))
        keep = ctx.enter_context(tc.tile_pool(name="keep", bufs=1))
        small = ctx.enter_context(tc.tile_pool(name="small", bufs=6))
        h_stage = ctx.enter_context(tc.tile_pool(name="h_stage", bufs=PASSES))
        w_raw = ctx.enter_context(tc.tile_pool(name="w_raw", bufs=3 * HALVES))
        w_stage = ctx.enter_context(tc.tile_pool(name="w_stage", bufs=2 * QUARTERS))
        out_stage = ctx.enter_context(tc.tile_pool(name="out_stage", bufs=8))
        scrap = ctx.enter_context(tc.tile_pool(name="scrap", bufs=4))
        sums_low = ctx.enter_context(tc.psum_pool(name="sums_low", bufs=4))
        ctx.enter_context(tc.manual_schedule())

        batches = range(BATCH)
        x_sb = [keep.tile([P, POS_TILES, CHAN], BF16, name="x_sb%d" % b) for b in batches]
        x_words = [keep.tile([P, POS_TILES, BLOCKS, P], F32, name="x_words%d" % b) for b in batches]
        chunk_stats = [keep.tile([P, BLOCKS, CHUNKS, STATS], F32, name="chunk_stats%d" % b) for b in batches]
        moments = [keep.tile([P, BLOCKS, 2], F32, name="moments%d" % b) for b in batches]
        gain = [keep.tile([P, BLOCKS, 2], F32, name="gain%d" % b) for b in batches]
        shift = [keep.tile([P, BLOCKS, 2], F32, name="shift%d" % b) for b in batches]
        h_planes, h_codes, h_scales = {}, {}, {}
        for b in batches:
            for c in range(PASSES):
                h_planes[b, c] = keep.tile([P, PACK, SEQ], BF16, name="h_planes%d%d" % (b, c))
                h_codes[b, c] = keep.tile([P, SEQ], U32, name="h_codes%d%d" % (b, c), align_bytes=64)
                h_scales[b, c] = keep.tile([P, SEQ], U8, name="h_scales%d%d" % (b, c), align_bytes=64)
        w_codes, w_scales = {}, {}
        for w in (Q, K, V):
            for quarter in range(QUARTERS):
                w_codes[w, quarter] = keep.tile([P, BANK], U32, name="w_codes%d%d" % (w, quarter), align_bytes=64)
                w_scales[w, quarter] = keep.tile([P, BANK], U8, name="w_scales%d%d" % (w, quarter), align_bytes=64)

        for b in batches:
            x_rows = x[b].rearrange("(p j) c -> p j c", j=POS_TILES)
            for chunk in range(CHUNKS):
                js = slice(CHUNK_TILES * chunk, CHUNK_TILES * (chunk + 1))
                nc.sync.dma_start(out=x_sb[b][:, js, :], in_=x_rows[:, js, :])
        affine_rows = const.tile([P, 2 * P], BF16)
        nc.vector.memset(affine_rows[:], 0.0)
        nc.sync.dma_start(out=affine_rows[0:BLOCKS, :], in_=gn1_g.rearrange("(a c) -> a c", a=BLOCKS))
        nc.sync.dma_start(out=affine_rows[BLOCKS : 2 * BLOCKS, :], in_=gn1_b.rearrange("(a c) -> a c", a=BLOCKS))
        w_sb = {}

        def load_w(w):
            w_rows = weights[w].rearrange("(h p i) k -> h p i k", h=HALVES, i=ROWS)
            for half in range(HALVES):
                w_sb[w, half] = w_raw.tile([P, ROWS, CHAN], BF16, name="w_sb")
                nc.sync.dma_start(out=w_sb[w, half][:], in_=w_rows[half])

        for w in (V, Q, K):
            load_w(w)

        ident = const.tile([P, P], F32)
        make_identity(nc, ident[:])
        group_avg = const.tile([P, P], F32)
        nc.vector.memset(group_avg[:], 0.0)
        for quad in range(P // QUAD):
            span = slice(QUAD * quad, QUAD * (quad + 1))
            nc.vector.memset(group_avg[span, span], 1.0 / QUAD)
        eps_gn = const.tile([P, 1], F32)
        nc.vector.memset(eps_gn[:], EPS_GN)
        warm = const.tile([P, 1], F32)
        nc.scalar.activation(out=warm[:], in_=eps_gn[:], func=ACT.Abs_reciprocal_sqrt)
        affine = const.tile([P, 2, BLOCKS, 2], F32)

        def block_statistics(b, chunk, a):
            js = slice(CHUNK_TILES * chunk, CHUNK_TILES * (chunk + 1))
            nc.vector.bn_stats(out=chunk_stats[b][:, a, chunk, :], in_=x_words[b][:, js, a, :].bitcast(BF16))

        def aggregate(b):
            for a in range(BLOCKS):
                nc.vector.bn_aggr(out=moments[b][:, a, :], in_=chunk_stats[b][:, a].rearrange("p n m -> p (n m)"))

        def square_means(b):
            squared = small.tile([P, BLOCKS], F32, name="squared")
            nc.vector.tensor_tensor(out=squared[:], in0=moments[b][:, :, 0], in1=moments[b][:, :, 0], op=ALU.mult)
            return squared

        def means_of_squares(b, squared):
            nc.vector.tensor_tensor(out=moments[b][:, :, 1], in0=moments[b][:, :, 1], in1=squared[:], op=ALU.add)

        def group_moments(b, columns):
            nc.tensor.matmul(
                out=columns, lhsT=group_avg[:], rhs=moments[b][:].rearrange("p a m -> p (a m)"), start=True, stop=True
            )
            both = columns.rearrange("p (a m) -> p a m", m=2)
            squared_mean = small.tile([P, BLOCKS], F32, name="squared_mean")
            nc.scalar.activation(out=squared_mean[:], in_=both[:, :, 0], func=ACT.Square)
            return both[:, :, 0], both[:, :, 1], squared_mean

        def group_rstd(mean_of_squares, squared_mean):
            var = small.tile([P, BLOCKS], F32, name="var")
            nc.vector.tensor_tensor(out=var[:], in0=mean_of_squares, in1=squared_mean[:], op=ALU.subtract)
            rstd = small.tile([P, BLOCKS], F32, name="rstd")
            nc.scalar.activation(out=rstd[:], in_=var[:], func=ACT.Abs_reciprocal_sqrt, bias=eps_gn[:, 0:1])
            return rstd

        by_channel = [P, BLOCKS, 2]

        def gains(b, rstd):
            nc.vector.tensor_tensor(
                out=gain[b][:], in0=affine[:, 0], in1=rstd[:].unsqueeze(2).to_broadcast(by_channel), op=ALU.mult
            )

        def moves(b, mean):
            moved = small.tile(by_channel, F32, name="moved")
            nc.vector.tensor_tensor(
                out=moved[:], in0=gain[b][:], in1=mean.unsqueeze(2).to_broadcast(by_channel), op=ALU.mult
            )
            return moved

        def shifts(b, moved):
            nc.vector.tensor_tensor(out=shift[b][:], in0=affine[:, 1], in1=moved[:], op=ALU.subtract)

        def normalise(engine, b, a):
            channels = x_words[b][:, :, a, :].bitcast(BF16).rearrange("p j (s e) -> p j s e", e=2)
            for e in range(2):
                engine.tensor_scalar(
                    out=h_planes[b, a // 2][:, 2 * (a % 2) + e, :].rearrange("p (j s) -> p j s", j=POS_TILES),
                    in0=channels[:, :, :, e],
                    scalar1=gain[b][:, a, e : e + 1],
                    scalar2=shift[b][:, a, e : e + 1],
                    op0=ALU.mult,
                    op1=ALU.add,
                )

        def regroup_h(b, c):
            grouped = h_stage.tile([P, SEQ, PACK], BF16, name="h_grouped", align_bytes=64)
            nc.vector.tensor_copy(
                out=grouped[:].rearrange("p (g r) t -> p g t r", r=RUN),
                in_=h_planes[b, c][:].rearrange("p t (g r) -> p g t r", r=RUN),
            )
            return grouped

        def quantise_h(b, c, grouped):
            nc.vector.quantize_mx(
                out=h_codes[b, c][:].bitcast(FP8X4),
                scales=h_scales[b, c][:],
                in_=grouped[:].rearrange("p s t -> p (s t)"),
            )

        w_grouped = {}

        def quantise_w(w, quarter):
            nc.vector.quantize_mx(
                out=w_codes[w, quarter][:].bitcast(FP8X4),
                scales=w_scales[w, quarter][:],
                in_=w_grouped[w, quarter][:],
            )

        tiles = [(V, 0, j) for j in range(POS_TILES - 1)]
        tiles.extend([(w, 0, j) for w in (Q, K) for j in range(POS_TILES)])
        tiles.append((V, 0, POS_TILES - 1))
        tiles.extend([(w, 1, j) for j in range(POS_TILES) for w in (Q, K, V)])
        accs, square_sums, inverses, results = {}, {}, {}, {}

        def multiply(n, pool):
            w, b, j = tiles[n]
            accs[n] = [pool.tile([P, BANK], F32, name="acc") for half in range(HALVES)]
            positions = slice(P * j, P * (j + 1))
            for half in range(HALVES):
                for c in range(PASSES):
                    nc.tensor.matmul_mx(
                        out=accs[n][half][:],
                        lhsT=h_codes[b, c][:, positions].bitcast(FP8X4),
                        lhsT_scale=h_scales[b, c][:, positions],
                        rhs=w_codes[w, PASSES * half + c][:].bitcast(FP8X4),
                        rhs_scale=w_scales[w, PASSES * half + c][:],
                        start=(c == 0),
                        stop=(c == PASSES - 1),
                    )

        def square(n, half):
            if tiles[n][0] == V:
                return
            if half == 0:
                square_sums[n] = small.tile([P, HALVES], F32, name="square_sums")
            squares = scrap.tile([P, BANK], BF16, name="squares")
            nc.scalar.activation(
                out=squares[:],
                in_=accs[n][half][:],
                func=ACT.Square,
                accum_out=square_sums[n][:, half : half + 1],
            )

        unclamped = {}

        def root(n):
            if tiles[n][0] == V:
                return
            unclamped[n] = small.tile([P, 1], F32, name="unclamped")
            nc.scalar.activation(
                out=unclamped[n][:],
                in_=square_sums[n][:, 0:1],
                func=ACT.Abs_reciprocal_sqrt,
                bias=square_sums[n][:, 1:2],
            )

        def clamp(n):
            if tiles[n][0] == V:
                return
            inverses[n] = small.tile([P, 1], F32, name="inverse")
            nc.vector.tensor_scalar_min(out=inverses[n][:], in0=unclamped[n][:], scalar1=1.0 / EPS_L2)

        def who(n, half):
            w, b, j = tiles[n]
            if w == V:
                return "S" if b == 0 else "SV"[half]
            return "SV"[half] if (w, b) == (K, 0) and j < CHUNK_TILES else "V"

        def leave_psum(n, half, engine):
            w, b, j = tiles[n]
            if n not in results:
                results[n] = out_stage.tile([P, HALVES, BANK], F32, name="result")
            in_order = accs[n][half][:].rearrange("s (i p) -> s p i", i=ROWS)
            result = results[n][:, half, :].rearrange("s (p i) -> s p i", i=ROWS)
            if w != V and engine == "V":
                nc.vector.tensor_scalar(
                    out=result, in0=in_order, scalar1=inverses[n][:, 0:1], scalar2=None, op0=ALU.mult
                )
            elif w != V:
                nc.scalar.activation(out=result, in_=in_order, func=ACT.Copy, scale=inverses[n][:, 0:1])
            elif engine == "S":
                nc.scalar.copy(out=result, in_=in_order)
            else:
                nc.vector.tensor_copy(out=result, in_=in_order)

        def store(n):
            w, b, j = tiles[n]
            out_rows = outs[w][b].rearrange("(p j) o -> j p o", j=POS_TILES)
            nc.sync.dma_start(out=out_rows[j], in_=results[n][:].rearrange("p h o -> p (h o)"))

        pools = [sums_low]
        grouped_h1 = {}
        first_h1_job = tiles.index((K, 0, POS_TILES - 1)) - 2 * PASSES

        def step(n):
            if n < len(tiles):
                multiply(n, pools[n % len(pools)])
            for half in range(HALVES):
                if n < len(tiles):
                    square(n, half)
                    if tiles[n][0] == V and who(n, half) == "S":
                        leave_psum(n, half, "S")
                if half == 0 and 0 <= n - 1 < len(tiles):
                    root(n - 1)
            if n < len(tiles) and tiles[n][0] == V and all(who(n, half) == "S" for half in range(HALVES)):
                store(n)
            m = n - LAG
            if 0 <= m - first_h1_job < 2 * PASSES:
                c, quantise = divmod(m - first_h1_job, 2)
                if quantise:
                    quantise_h(1, c, grouped_h1[c])
                else:
                    grouped_h1[c] = regroup_h(1, c)
            if 0 <= m < len(tiles):
                late = [half for half in range(HALVES) if tiles[m][0] != V or who(m, half) == "V"]
                for half in late[:-1]:
                    leave_psum(m, half, who(m, half))
            if 0 <= m + 1 < len(tiles):
                clamp(m + 1)
            if 0 <= m < len(tiles):
                for half in late[-1:]:
                    leave_psum(m, half, who(m, half))
                    store(m)

        with tc.psum_pool(name="turned", bufs=4) as turned:

            def transpose_x(b, j):
                x_t = turned.tile([P, BANK], F32, name="x_t", tag="turned")
                words = x_sb[b][:, j, :].bitcast(F32)
                for a in range(BLOCKS):
                    cols = slice(P * a, P * (a + 1))
                    nc.tensor.transpose(x_t[:, cols], words[:, cols], ident[:])
                nc.scalar.copy(out=x_words[b][:, j].rearrange("p a s -> p (a s)"), in_=x_t[:])

            def transpose_w(w, quarter):
                half, c = quarter // PASSES, quarter % PASSES
                grouped = w_stage.tile([P, BANK * PACK], BF16, name="w_grouped", align_bytes=64)
                grouped_words = grouped[:].bitcast(F32).rearrange("p (o u) -> p o u", u=2)
                width = BANK_ROWS * P
                for bank in range(ROWS // BANK_ROWS):
                    w_t = turned.tile([P, BANK], F32, name="w_t", tag="turned")
                    for u in range(2):
                        for r in range(BANK_ROWS):
                            words = w_sb[w, half][:, BANK_ROWS * bank + r, :].bitcast(F32)
                            a = 2 * c + u
                            nc.tensor.transpose(
                                w_t[:, width * u + P * r : width * u + P * (r + 1)],
                                words[:, P * a : P * (a + 1)],
                                ident[:],
                            )
                    nc.scalar.copy(
                        out=grouped_words[:, width * bank : width * (bank + 1), :],
                        in_=w_t[:].rearrange("p (u o) -> p o u", u=2),
                    )
                w_grouped[w, quarter] = grouped

            for j in range(POS_TILES):
                transpose_x(0, j)
                if j % CHUNK_TILES == CHUNK_TILES - 1:
                    for a in range(BLOCKS):
                        block_statistics(0, j // CHUNK_TILES, a)
            for j in range(POS_TILES):
                transpose_x(1, j)
            affine_t = turned.tile([P, BANK], F32, name="affine_t", tag="turned")
            nc.tensor.transpose(affine_t[:, 0:P], affine_rows[:].bitcast(F32), ident[:])
            aggregate(0)
            nc.vector.tensor_copy(
                out=affine[:].rearrange("p v a e -> p (v a e)"),
                in_=affine_t[:, 0 : 2 * BLOCKS].bitcast(BF16),
            )
            squared = square_means(0)
            transpose_w(V, 0)
            transpose_w(V, 1)
            block_statistics(1, 0, 0)
            means_of_squares(0, squared)
            group_t = turned.tile([P, BANK], F32, name="group_t", tag="turned")
            mean, mean_of_squares, squared_mean = group_moments(0, group_t[:, 0 : 2 * BLOCKS])
            transpose_w(V, 2)
            for a in range(1, BLOCKS):
                block_statistics(1, 0, a)
            rstd = group_rstd(mean_of_squares, squared_mean)
            transpose_w(V, 3)
            quantise_w(V, 0)
            gains(0, rstd)
            quantise_w(V, 1)
            moved = moves(0, mean)
            quantise_w(V, 2)
            shifts(0, moved)
            quantise_w(V, 3)
            for quarter in range(QUARTERS):
                transpose_w(Q, quarter)
            normalise(nc.vector, 0, 0)
            normalise(nc.vector, 0, 1)
            normalise(nc.vector, 0, 2)
            grouped_0 = regroup_h(0, 0)
            normalise(nc.vector, 0, 3)
            quantise_h(0, 0, grouped_0)
            grouped_1 = regroup_h(0, 1)
            block_statistics(1, 1, 0)
            quantise_h(0, 1, grouped_1)
            for quarter in range(QUARTERS):
                transpose_w(K, quarter)
            for a in range(1, BLOCKS):
                block_statistics(1, 1, a)
            aggregate(1)
            step(0)
            step(1)
            quantise_w(Q, 0)
            squared = square_means(1)
            quantise_w(Q, 1)
            means_of_squares(1, squared)
            group_t = turned.tile([P, BANK], F32, name="group_t", tag="turned")
            mean, mean_of_squares, squared_mean = group_moments(1, group_t[:, 0 : 2 * BLOCKS])
            quantise_w(Q, 2)
            step(2)
            rstd = group_rstd(mean_of_squares, squared_mean)
            quantise_w(Q, 3)
            quantise_w(K, 0)
            gains(1, rstd)
            quantise_w(K, 1)
            moved = moves(1, mean)
            quantise_w(K, 2)
            shifts(1, moved)
            quantise_w(K, 3)
        pools.append(ctx.enter_context(tc.psum_pool(name="sums_high", bufs=4, reuse_waits="tile")))
        for a in range(BLOCKS):
            normalise(nc.gpsimd, 1, a)
        for n in range(3, len(tiles) + LAG):
            step(n)
